import numpy as np
import ml_dtypes


def mxq(x, axis, fmt="e4m3"):
    dtype, down = {"e4m3": (ml_dtypes.float8_e4m3fn, 7), "e5m2": (ml_dtypes.float8_e5m2, 14)}[fmt]
    v = np.moveaxis(np.asarray(x, np.float32).astype(ml_dtypes.bfloat16).astype(np.float64), axis, -1)
    blocks = v.reshape(v.shape[:-1] + (-1, 32))
    amax = np.abs(blocks).max(-1, keepdims=True)
    byte = np.maximum(np.where(amax > 0, np.frexp(amax)[1] - 1 + 127, 0) - down, 1)
    scale = np.exp2(byte - 127.0)
    codes = (blocks / scale).astype(np.float32).astype(dtype).astype(np.float64)
    return np.moveaxis((codes * scale).reshape(v.shape), -1, axis)


WIDE = False


def mx_kscale(k):
    if not WIDE:
        return np.ones(k)
    levels = np.array([10, -10, 5, -5, 0])
    a = np.random.permutation(np.resize(levels, k // 512 * 4)).reshape(k // 512, 4)
    idx = np.arange(k)
    return np.exp2(a[idx // 512, idx % 128 // 32])


BF16 = ml_dtypes.bfloat16


def bf(x):
    return np.asarray(x, np.float32).astype(BF16)


def f64(x):
    return np.asarray(x).astype(np.float64)


R, C, E, H = 16, 512, 512, 4
D = E // H
RD = R * D


def setup_inputs():
    s = mx_kscale(E)
    return {"attn_weights": bf(np.random.standard_normal((H, C, C)) * 2.0),
            "mask0": bf(np.random.uniform(size=C) < 0.1),
            "x": bf(np.random.standard_normal((R, C, E)) * s),
            "Wv": bf(np.random.standard_normal((E, E)) * 2.0 / np.sqrt(E) / s[:, None]),
            "bv": bf(np.random.standard_normal(E) * 0.1)}


def reference(attn_weights, mask0, x, Wv, bv):
    m0 = f64(mask0)[None, :, None]
    a = f64(attn_weights) * (1.0 - m0) + m0 * (-10000.0)
    e = np.exp(a - a.max(-1, keepdims=True))
    p = e / e.sum(-1, keepdims=True)
    v = (mxq(f64(x), 2, "e4m3") @ mxq(f64(Wv), 0, "e4m3")) + f64(bv)
    vm = v.reshape(R, C, H, D).transpose(2, 1, 0, 3).reshape(H, C, RD)
    ctx = mxq(p, 2, "e4m3") @ mxq(vm, 1, "e4m3")
    return ctx.reshape(H, C, R, D).transpose(2, 1, 0, 3).reshape(R, C, E)

@@ -1,0 +1,332 @@
+from contextlib import ExitStack
+
+import concourse.mybir as mybir
+from concourse.masks import make_identity
+
+F32 = mybir.dt.float32
+BF16 = mybir.dt.bfloat16
+U32 = mybir.dt.uint32
+U8 = mybir.dt.uint8
+FP8X4 = mybir.dt.float8_e4m3fn_x4
+ALU = mybir.AluOpType
+ACT = mybir.ActivationFunctionType
+AXIS = mybir.AxisListType
+
+P = 128
+PACK = 4
+R, C, E, H = 16, 512, 512, 4
+D = E // H
+QUERY_TILES = C // P
+X_BANKS = 2
+AHEAD = 2
+BEHIND = 2
+
+FLOPS = 2 * R * C * E * E + 2 * H * C * C * R * D
+
+
+def tile_rowselfattention_pb_t_kernel(tc, attn_weights, mask0, x, Wv, bv, out):
+    nc = tc.nc
+    with ExitStack() as ctx:
+        const = ctx.enter_context(tc.tile_pool(name="const", bufs=1))
+        x_pool = ctx.enter_context(tc.tile_pool(name="x_pool", bufs=R))
+        x_stage = ctx.enter_context(tc.tile_pool(name="x_stage", bufs=3))
+        x_mx = ctx.enter_context(tc.tile_pool(name="x_mx", bufs=AHEAD + 2))
+        v_stage = ctx.enter_context(tc.tile_pool(name="v_stage", bufs=3))
+        v_mx = ctx.enter_context(tc.tile_pool(name="v_mx", bufs=BEHIND + 2))
+        psum_x = ctx.enter_context(tc.psum_pool(name="psum_x", bufs=X_BANKS))
+        psum_v = ctx.enter_context(tc.psum_pool(name="psum_v", bufs=3))
+        psum_o = ctx.enter_context(tc.psum_pool(name="psum_o", bufs=3))
+        ctx.enter_context(tc.manual_schedule())
+
+        ident_f32 = const.tile([P, P], F32)
+        make_identity(nc, ident_f32[:])
+        ident_bf16 = const.tile([P, P], BF16)
+        make_identity(nc, ident_bf16[:])
+        ones = const.tile([P, P], BF16)
+        nc.vector.memset(ones[:], 1.0)
+        bias_row = const.tile([P, E], BF16)
+        nc.vector.memset(bias_row[:], 0.0)
+        zero = const.tile([P, 1], F32)
+        nc.vector.memset(zero[:], 0.0)
+        one = const.tile([P, 1], F32)
+
+        bias_sb = const.tile([P, E], F32)
+        w_codes = const.tile([P, E], U32, align_bytes=64)
+        w_scales = const.tile([P, E], U8, align_bytes=64)
+        p_codes = const.tile([P, H * C], U32, align_bytes=64)
+        p_scales = const.tile([P, H * C], U8, align_bytes=64)
+        mask_sb = const.tile([P, QUERY_TILES], BF16)
+        keep = const.tile([P, QUERY_TILES], F32)
+        row_max = const.tile([P, H * QUERY_TILES], F32)
+        shift = const.tile([P, H * QUERY_TILES], F32)
+        row_sum = const.tile([P, H * QUERY_TILES], F32)
+        inv_sum = const.tile([P, H * QUERY_TILES], F32)
+
+        x_tiles = {}
+        x_ps_tiles = {}
+        x_grouped_tiles = {}
+        x_mx_tiles = {}
+
+        def load_x(r):
+            x_sb = x_pool.tile([P, PACK * E], BF16)
+            nc.sync.dma_start(out=x_sb[:], in_=x[r].rearrange("(q t) f -> q (t f)", t=PACK))
+            x_tiles[r] = x_sb
+
+        def x_transpose(r):
+            words = x_tiles[r][:].bitcast(F32)
+            x_ps_tiles[r] = []
+            for bank in range(X_BANKS):
+                x_ps = psum_x.tile([P, 2, 2, P], F32)
+                for t_in in range(2):
+                    for u in range(2):
+                        first = ((2 * bank + t_in) * 2 + u) * P
+                        nc.tensor.transpose(x_ps[:, t_in, u, :], words[:, first : first + P], ident_f32[:])
+                x_ps_tiles[r].append(x_ps)
+
+        def x_evacuate(r):
+            x_grouped = x_stage.tile([P, PACK * P * PACK], BF16, align_bytes=64)
+            grouped_words = x_grouped[:].bitcast(F32).rearrange("w (t q u) -> w t q u", t=PACK, u=2)
+            for bank in range(X_BANKS):
+                nc.scalar.copy(
+                    out=grouped_words[:, 2 * bank : 2 * bank + 2],
+                    in_=x_ps_tiles[r][bank][:].rearrange("w t u q -> w t q u"),
+                )
+            x_grouped_tiles[r] = x_grouped
+
+        def x_quantise(r):
+            x_codes = x_mx.tile([P, PACK * P], U32, align_bytes=64)
+            x_scales = x_mx.tile([P, PACK * P], U8, align_bytes=64)
+            nc.vector.quantize_mx(
+                out=x_codes[:].bitcast(FP8X4), scales=x_scales[:], in_=x_grouped_tiles[r][:]
+            )
+            x_mx_tiles[r] = (x_codes, x_scales)
+
+        v_grouped_tiles = {}
+        v_mx_tiles = {}
+
+        def project_bank(r, h):
+            if h == 0:
+                v_grouped = v_stage.tile([P, H, D, PACK], BF16, align_bytes=64)
+                v_grouped_tiles[r] = v_grouped
+            x_codes, x_scales = x_mx_tiles[r]
+            head = slice(h * D, (h + 1) * D)
+            v_ps = psum_v.tile([P, PACK, D], F32)
+            for t in range(PACK):
+                cols = slice(t * P, (t + 1) * P)
+                nc.tensor.matmul_mx(
+                    out=v_ps[:, t, :],
+                    lhsT=x_codes[:, cols].bitcast(FP8X4),
+                    lhsT_scale=x_scales[:, cols],
+                    rhs=w_codes[:, head].bitcast(FP8X4),
+                    rhs_scale=w_scales[:, head],
+                    start=True,
+                    stop=True,
+                )
+            nc.vector.tensor_tensor(
+                out=v_grouped_tiles[r][:, h],
+                in0=v_ps[:].rearrange("q t d -> q d t"),
+                in1=bias_sb[:, head].unsqueeze(2).to_broadcast([P, D, PACK]),
+                op=ALU.add,
+            )
+
+        def v_quantise(r):
+            v_codes = v_mx.tile([P, E], U32, align_bytes=64)
+            v_scales = v_mx.tile([P, E], U8, align_bytes=64)
+            nc.vector.quantize_mx(
+                out=v_codes[:].bitcast(FP8X4),
+                scales=v_scales[:],
+                in_=v_grouped_tiles[r][:].rearrange("q h d t -> q (h d t)"),
+            )
+            v_mx_tiles[r] = (v_codes, v_scales)
+
+        with ExitStack() as start:
+            attn_pool = start.enter_context(tc.tile_pool(name="attn_pool", bufs=H))
+            w_pool = start.enter_context(tc.tile_pool(name="w_pool", bufs=1))
+            max_pool = start.enter_context(tc.tile_pool(name="max_pool", bufs=2))
+            exp_pool = start.enter_context(tc.tile_pool(name="exp_pool", bufs=2 * QUERY_TILES))
+            p_pool = start.enter_context(tc.tile_pool(name="p_pool", bufs=QUERY_TILES))
+            p_stage = start.enter_context(tc.tile_pool(name="p_stage", bufs=2))
+
+            nc.scalar.dma_start(out=mask_sb[:], in_=mask0.rearrange("(m s) -> m s", s=QUERY_TILES))
+            nc.scalar.dma_start(out=bias_row[0:1, :], in_=bv.rearrange("(o e) -> o e", o=1))
+            nc.scalar.activation(out=one[:], in_=zero[:], func=ACT.Exp)
+            attn_tiles = {}
+
+            def load_attn(h):
+                attn_sb = attn_pool.tile([P, QUERY_TILES, C], BF16)
+                nc.sync.dma_start(
+                    out=attn_sb[:].rearrange("m s j -> m (s j)"),
+                    in_=attn_weights[h].rearrange("(m s) j -> m (s j)", s=QUERY_TILES),
+                )
+                attn_tiles[h] = attn_sb
+
+            load_attn(0)
+            load_attn(1)
+            w_rows = w_pool.tile([P, PACK, E], BF16)
+            nc.sync.dma_start(
+                out=w_rows[:].rearrange("w (u e) n -> w u (e n)", u=2),
+                in_=Wv.rearrange("(u w e) n -> w u (e n)", u=2, e=2),
+            )
+            load_x(0)
+            load_x(1)
+            load_attn(2)
+            load_attn(3)
+            for r in range(2, R):
+                load_x(r)
+
+            def prepare_weights():
+                w_grouped = w_pool.tile([P, E, PACK], BF16, align_bytes=64)
+                nc.vector.tensor_copy(out=w_grouped[:], in_=w_rows[:].rearrange("w t n -> w n t"))
+                nc.vector.quantize_mx(
+                    out=w_codes[:].bitcast(FP8X4),
+                    scales=w_scales[:],
+                    in_=w_grouped[:].rearrange("w n t -> w (n t)"),
+                )
+
+            def prepare_bias():
+                bias_ps = psum_v.tile([P, E], F32, tag="v_ps")
+                nc.tensor.matmul(out=bias_ps[:], lhsT=ones[:], rhs=bias_row[:], start=True, stop=True)
+                nc.scalar.copy(out=bias_sb[:], in_=bias_ps[:])
+
+            nc.vector.tensor_scalar(
+                out=keep[:], in0=mask_sb[:], scalar1=-1.0, scalar2=1.0, op0=ALU.mult, op1=ALU.add
+            )
+            exp_tiles = {}
+            p_grouped_tiles = {}
+
+            def softmax_max(h):
+                cols = slice(h * QUERY_TILES, (h + 1) * QUERY_TILES)
+                attn_sb = attn_tiles[h]
+                half_max = max_pool.tile([P, QUERY_TILES, C // 2], BF16)
+                nc.vector.tensor_max(
+                    out=half_max[:], in0=attn_sb[:, :, 0 : C // 2], in1=attn_sb[:, :, C // 2 : C]
+                )
+                quarter_max = max_pool.tile([P, QUERY_TILES, C // 4], BF16)
+                nc.vector.tensor_max(
+                    out=quarter_max[:], in0=half_max[:, :, 0 : C // 4], in1=half_max[:, :, C // 4 : C // 2]
+                )
+                nc.vector.tensor_reduce(out=row_max[:, cols], in_=quarter_max[:], axis=AXIS.X, op=ALU.max)
+                nc.vector.scalar_tensor_tensor(
+                    out=shift[:, cols], in0=row_max[:, cols], scalar=-1.0, in1=keep[:],
+                    op0=ALU.mult, op1=ALU.mult,
+                )
+
+            def softmax_exp(h):
+                for s in range(QUERY_TILES):
+                    col = h * QUERY_TILES + s
+                    exp_sb = exp_pool.tile([P, PACK, P], F32)
+                    nc.scalar.activation(
+                        out=exp_sb[:],
+                        in_=attn_tiles[h][:, s, :].rearrange("m (q t) -> m t q", t=PACK),
+                        func=ACT.Exp,
+                        bias=shift[:, col : col + 1],
+                        scale=keep[:, s : s + 1],
+                        accum_out=row_sum[:, col : col + 1],
+                    )
+                    exp_tiles[(h, s)] = exp_sb
+
+            def softmax_transpose(h):
+                cols = slice(h * QUERY_TILES, (h + 1) * QUERY_TILES)
+                nc.vector.reciprocal(out=inv_sum[:, cols], in_=row_sum[:, cols])
+                p_grouped = p_stage.tile([P, QUERY_TILES, P, PACK], BF16, align_bytes=64)
+                for s in range(QUERY_TILES):
+                    col = h * QUERY_TILES + s
+                    p_sb = p_pool.tile([P, PACK, P], BF16)
+                    nc.vector.tensor_scalar(
+                        out=p_sb[:], in0=exp_tiles[(h, s)][:], scalar1=inv_sum[:, col : col + 1],
+                        scalar2=None, op0=ALU.mult,
+                    )
+                    p_ps = psum_o.tile([P, PACK, P], BF16, tag="o_ps")
+                    for t in range(PACK):
+                        nc.tensor.transpose(p_ps[:, t, :], p_sb[:, t, :], ident_bf16[:])
+                    nc.scalar.copy(out=p_grouped[:, s], in_=p_ps[:].rearrange("q t m -> q m t"))
+                p_grouped_tiles[h] = p_grouped
+
+            def softmax_quantise(h):
+                cols = slice(h * C, (h + 1) * C)
+                nc.vector.quantize_mx(
+                    out=p_codes[:, cols].bitcast(FP8X4),
+                    scales=p_scales[:, cols],
+                    in_=p_grouped_tiles[h][:].rearrange("q s m t -> q (s m t)"),
+                )
+
+            first_rows = AHEAD + BEHIND
+            softmax_max(0)
+            prepare_bias()
+            softmax_max(1)
+            prepare_weights()
+            x_transpose(0)
+            for k in range(H + 2):
+                if k < H:
+                    softmax_exp(k)
+                if k < first_rows:
+                    x_evacuate(k)
+                if k + 2 < H:
+                    softmax_max(k + 2)
+                if 0 <= k - 1 < first_rows:
+                    x_quantise(k - 1)
+                if 0 <= k - 2 < BEHIND:
+                    for h in range(H):
+                        project_bank(k - 2, h)
+                if 0 <= k - 1 < H:
+                    softmax_transpose(k - 1)
+                if 0 <= k - 2 < BEHIND:
+                    v_quantise(k - 2)
+                if 0 <= k - 2 < H:
+                    softmax_quantise(k - 2)
+                if k + 1 < first_rows:
+                    x_transpose(k + 1)
+
+        out_pool = ctx.enter_context(tc.tile_pool(name="out_pool", bufs=5))
+        out_tiles = {}
+
+        def attend_bank(bank, copy):
+            r, s = divmod(bank, QUERY_TILES)
+            if s == 0:
+                out_sb = out_pool.tile([P, QUERY_TILES, E], F32)
+                out_tiles[r] = out_sb
+            v_codes, v_scales = v_mx_tiles[r]
+            o_ps = psum_o.tile([P, E], F32)
+            for h in range(H):
+                queries = slice((h * QUERY_TILES + s) * P, (h * QUERY_TILES + s + 1) * P)
+                head = slice(h * D, (h + 1) * D)
+                nc.tensor.matmul_mx(
+                    out=o_ps[:, head],
+                    lhsT=p_codes[:, queries].bitcast(FP8X4),
+                    lhsT_scale=p_scales[:, queries],
+                    rhs=v_codes[:, head].bitcast(FP8X4),
+                    rhs_scale=v_scales[:, head],
+                    start=True,
+                    stop=True,
+                )
+            copy(out=out_tiles[r][:, s, :], in_=o_ps[:])
+            if s % 2 == 1:
+                nc.sync.dma_start(
+                    out=out[r].rearrange("(m s) e -> m s e", s=QUERY_TILES)[:, s - 1 : s + 1, :],
+                    in_=out_tiles[r][:, s - 1 : s + 1, :],
+                )
+
+        for r in range(BEHIND, R):
+            more_x = r + AHEAD < R
+            bank = QUERY_TILES * (r - BEHIND) + X_BANKS * max(0, r + AHEAD - R)
+            if more_x:
+                x_transpose(r + AHEAD)
+            project_bank(r, 0)
+            if more_x:
+                x_evacuate(r + AHEAD)
+            else:
+                for spare in range(X_BANKS):
+                    attend_bank(bank, nc.scalar.copy)
+                    bank += 1
+            for h in range(1, H + 1):
+                if h < H:
+                    project_bank(r, h)
+                attend_bank(bank, nc.scalar.copy)
+                bank += 1
+            if more_x:
+                x_quantise(r + AHEAD)
+            v_quantise(r)
+
+        for s in range(QUERY_TILES):
+            copy = nc.scalar.copy if s % 2 == 0 else nc.vector.tensor_copy
+            attend_bank(QUERY_TILES * (R - 1) + s, copy)

@@ -144,11 +144,11 @@ def tile_rowselfattention_pb_t_kernel(tc, attn_weights, mask0, x, Wv, bv, out):
             w_pool = start.enter_context(tc.tile_pool(name="w_pool", bufs=1))
             max_pool = start.enter_context(tc.tile_pool(name="max_pool", bufs=2))
             exp_pool = start.enter_context(tc.tile_pool(name="exp_pool", bufs=2 * QUERY_TILES))
-            p_pool = start.enter_context(tc.tile_pool(name="p_pool", bufs=QUERY_TILES))
-            p_stage = start.enter_context(tc.tile_pool(name="p_stage", bufs=2))
+            p_pool = start.enter_context(tc.tile_pool(name="p_pool", bufs=2 * QUERY_TILES))
+            p_stage = start.enter_context(tc.tile_pool(name="p_stage", bufs=H))
 
-            nc.scalar.dma_start(out=mask_sb[:], in_=mask0.rearrange("(m s) -> m s", s=QUERY_TILES))
-            nc.scalar.dma_start(out=bias_row[0:1, :], in_=bv.rearrange("(o e) -> o e", o=1))
+            nc.sync.dma_start(out=mask_sb[:], in_=mask0.rearrange("(m s) -> m s", s=QUERY_TILES))
+            nc.sync.dma_start(out=bias_row[0:1, :], in_=bv.rearrange("(o e) -> o e", o=1))
             nc.scalar.activation(out=one[:], in_=zero[:], func=ACT.Exp)
             attn_tiles = {}
 
@@ -192,20 +192,29 @@ def tile_rowselfattention_pb_t_kernel(tc, attn_weights, mask0, x, Wv, bv, out):
                 out=keep[:], in0=mask_sb[:], scalar1=-1.0, scalar2=1.0, op0=ALU.mult, op1=ALU.add
             )
             exp_tiles = {}
+            p_ps_tiles = {}
             p_grouped_tiles = {}
 
             def softmax_max(h):
                 cols = slice(h * QUERY_TILES, (h + 1) * QUERY_TILES)
                 attn_sb = attn_tiles[h]
+                halves = [slice(0, QUERY_TILES // 2), slice(QUERY_TILES // 2, QUERY_TILES)]
                 half_max = max_pool.tile([P, QUERY_TILES, C // 2], BF16)
-                nc.vector.tensor_max(
-                    out=half_max[:], in0=attn_sb[:, :, 0 : C // 2], in1=attn_sb[:, :, C // 2 : C]
-                )
+                for part in halves:
+                    nc.vector.tensor_max(
+                        out=half_max[:, part], in0=attn_sb[:, part, 0 : C // 2], in1=attn_sb[:, part, C // 2 : C]
+                    )
                 quarter_max = max_pool.tile([P, QUERY_TILES, C // 4], BF16)
-                nc.vector.tensor_max(
-                    out=quarter_max[:], in0=half_max[:, :, 0 : C // 4], in1=half_max[:, :, C // 4 : C // 2]
-                )
-                nc.vector.tensor_reduce(out=row_max[:, cols], in_=quarter_max[:], axis=AXIS.X, op=ALU.max)
+                for part in halves:
+                    nc.vector.tensor_max(
+                        out=quarter_max[:, part],
+                        in0=half_max[:, part, 0 : C // 4],
+                        in1=half_max[:, part, C // 4 : C // 2],
+                    )
+                for part in halves:
+                    nc.vector.tensor_reduce(
+                        out=row_max[:, cols][:, part], in_=quarter_max[:, part], axis=AXIS.X, op=ALU.max
+                    )
                 nc.vector.scalar_tensor_tensor(
                     out=shift[:, cols], in0=row_max[:, cols], scalar=-1.0, in1=keep[:],
                     op0=ALU.mult, op1=ALU.mult,
@@ -228,7 +237,7 @@ def tile_rowselfattention_pb_t_kernel(tc, attn_weights, mask0, x, Wv, bv, out):
             def softmax_transpose(h):
                 cols = slice(h * QUERY_TILES, (h + 1) * QUERY_TILES)
                 nc.vector.reciprocal(out=inv_sum[:, cols], in_=row_sum[:, cols])
-                p_grouped = p_stage.tile([P, QUERY_TILES, P, PACK], BF16, align_bytes=64)
+                p_ps_tiles[h] = []
                 for s in range(QUERY_TILES):
                     col = h * QUERY_TILES + s
                     p_sb = p_pool.tile([P, PACK, P], BF16)
@@ -236,10 +245,19 @@ def tile_rowselfattention_pb_t_kernel(tc, attn_weights, mask0, x, Wv, bv, out):
                         out=p_sb[:], in0=exp_tiles[(h, s)][:], scalar1=inv_sum[:, col : col + 1],
                         scalar2=None, op0=ALU.mult,
                     )
-                    p_ps = psum_o.tile([P, PACK, P], BF16, tag="o_ps")
+                    if s % 2 == 0:
+                        p_ps = psum_o.tile([P, 2, PACK, P], BF16, tag="o_ps")
+                        p_ps_tiles[h].append(p_ps)
                     for t in range(PACK):
-                        nc.tensor.transpose(p_ps[:, t, :], p_sb[:, t, :], ident_bf16[:])
-                    nc.scalar.copy(out=p_grouped[:, s], in_=p_ps[:].rearrange("q t m -> q m t"))
+                        nc.tensor.transpose(p_ps_tiles[h][s // 2][:, s % 2, t, :], p_sb[:, t, :], ident_bf16[:])
+
+            def softmax_evacuate(h):
+                p_grouped = p_stage.tile([P, QUERY_TILES, P, PACK], BF16, align_bytes=64)
+                for pair in range(QUERY_TILES // 2):
+                    nc.scalar.copy(
+                        out=p_grouped[:, 2 * pair : 2 * pair + 2],
+                        in_=p_ps_tiles[h][pair][:].rearrange("q s t m -> q s m t"),
+                    )
                 p_grouped_tiles[h] = p_grouped
 
             def softmax_quantise(h):
@@ -252,39 +270,37 @@ def tile_rowselfattention_pb_t_kernel(tc, attn_weights, mask0, x, Wv, bv, out):
 
             first_rows = AHEAD + BEHIND
             softmax_max(0)
-            prepare_bias()
             softmax_max(1)
+            prepare_bias()
             prepare_weights()
             x_transpose(0)
-            for k in range(H + 2):
+            for k in range(H + 3):
+                if 0 <= k - 2 < H:
+                    softmax_evacuate(k - 2)
                 if k < H:
                     softmax_exp(k)
                 if k < first_rows:
                     x_evacuate(k)
-                if k + 2 < H:
-                    softmax_max(k + 2)
+                if 0 <= k - 1 < H:
+                    softmax_transpose(k - 1)
+                if 2 <= k + 1 < H:
+                    softmax_max(k + 1)
                 if 0 <= k - 1 < first_rows:
                     x_quantise(k - 1)
                 if 0 <= k - 2 < BEHIND:
                     for h in range(H):
                         project_bank(k - 2, h)
-                if 0 <= k - 1 < H:
-                    softmax_transpose(k - 1)
-                if 0 <= k - 2 < BEHIND:
-                    v_quantise(k - 2)
-                if 0 <= k - 2 < H:
-                    softmax_quantise(k - 2)
                 if k + 1 < first_rows:
                     x_transpose(k + 1)
+                if 0 <= k - 3 < H:
+                    softmax_quantise(k - 3)
+                if 0 <= k - 3 < BEHIND:
+                    v_quantise(k - 3)
 
-        out_pool = ctx.enter_context(tc.tile_pool(name="out_pool", bufs=5))
-        out_tiles = {}
+        out_pool = ctx.enter_context(tc.tile_pool(name="out_pool", bufs=12))
 
         def attend_bank(bank, copy):
             r, s = divmod(bank, QUERY_TILES)
-            if s == 0:
-                out_sb = out_pool.tile([P, QUERY_TILES, E], F32)
-                out_tiles[r] = out_sb
             v_codes, v_scales = v_mx_tiles[r]
             o_ps = psum_o.tile([P, E], F32)
             for h in range(H):
@@ -299,12 +315,9 @@ def tile_rowselfattention_pb_t_kernel(tc, attn_weights, mask0, x, Wv, bv, out):
                     start=True,
                     stop=True,
                 )
-            copy(out=out_tiles[r][:, s, :], in_=o_ps[:])
-            if s % 2 == 1:
-                nc.sync.dma_start(
-                    out=out[r].rearrange("(m s) e -> m s e", s=QUERY_TILES)[:, s - 1 : s + 1, :],
-                    in_=out_tiles[r][:, s - 1 : s + 1, :],
-                )
+            out_sb = out_pool.tile([P, E], F32)
+            copy(out=out_sb[:], in_=o_ps[:])
+            nc.sync.dma_start(out=out[r].rearrange("(m s) e -> m s e", s=QUERY_TILES)[:, s, :], in_=out_sb[:])
 
         for r in range(BEHIND, R):
             more_x = r + AHEAD < R

@@ -151,13 +151,15 @@ def tile_rowselfattention_pb_t_kernel(tc, attn_weights, mask0, x, Wv, bv, out):
             nc.sync.dma_start(out=bias_row[0:1, :], in_=bv.rearrange("(o e) -> o e", o=1))
             nc.scalar.activation(out=one[:], in_=zero[:], func=ACT.Exp)
             attn_tiles = {}
+            halves = [slice(0, QUERY_TILES // 2), slice(QUERY_TILES // 2, QUERY_TILES)]
 
             def load_attn(h):
                 attn_sb = attn_pool.tile([P, QUERY_TILES, C], BF16)
-                nc.sync.dma_start(
-                    out=attn_sb[:].rearrange("m s j -> m (s j)"),
-                    in_=attn_weights[h].rearrange("(m s) j -> m (s j)", s=QUERY_TILES),
-                )
+                for part in halves:
+                    nc.sync.dma_start(
+                        out=attn_sb[:, part, :],
+                        in_=attn_weights[h].rearrange("(m s) j -> m s j", s=QUERY_TILES)[:, part, :],
+                    )
                 attn_tiles[h] = attn_sb
 
             load_attn(0)
@@ -198,7 +200,6 @@ def tile_rowselfattention_pb_t_kernel(tc, attn_weights, mask0, x, Wv, bv, out):
             def softmax_max(h):
                 cols = slice(h * QUERY_TILES, (h + 1) * QUERY_TILES)
                 attn_sb = attn_tiles[h]
-                halves = [slice(0, QUERY_TILES // 2), slice(QUERY_TILES // 2, QUERY_TILES)]
                 half_max = max_pool.tile([P, QUERY_TILES, C // 2], BF16)
                 for part in halves:
                     nc.vector.tensor_max(
@@ -215,10 +216,11 @@ def tile_rowselfattention_pb_t_kernel(tc, attn_weights, mask0, x, Wv, bv, out):
                     nc.vector.tensor_reduce(
                         out=row_max[:, cols][:, part], in_=quarter_max[:, part], axis=AXIS.X, op=ALU.max
                     )
-                nc.vector.scalar_tensor_tensor(
-                    out=shift[:, cols], in0=row_max[:, cols], scalar=-1.0, in1=keep[:],
-                    op0=ALU.mult, op1=ALU.mult,
-                )
+                for part in halves:
+                    nc.vector.scalar_tensor_tensor(
+                        out=shift[:, cols][:, part], in0=row_max[:, cols][:, part], scalar=-1.0, in1=keep[:, part],
+                        op0=ALU.mult, op1=ALU.mult,
+                    )
 
             def softmax_exp(h):
                 for s in range(QUERY_TILES):
@@ -297,10 +299,14 @@ def tile_rowselfattention_pb_t_kernel(tc, attn_weights, mask0, x, Wv, bv, out):
                 if 0 <= k - 3 < BEHIND:
                     v_quantise(k - 3)
 
-        out_pool = ctx.enter_context(tc.tile_pool(name="out_pool", bufs=12))
+        out_pool = ctx.enter_context(tc.tile_pool(name="out_pool", bufs=4))
+        out_tiles = {}
 
         def attend_bank(bank, copy):
             r, s = divmod(bank, QUERY_TILES)
+            if s == 0:
+                out_sb = out_pool.tile([P, QUERY_TILES, E], F32)
+                out_tiles[r] = out_sb
             v_codes, v_scales = v_mx_tiles[r]
             o_ps = psum_o.tile([P, E], F32)
             for h in range(H):
@@ -315,9 +321,10 @@ def tile_rowselfattention_pb_t_kernel(tc, attn_weights, mask0, x, Wv, bv, out):
                     start=True,
                     stop=True,
                 )
-            out_sb = out_pool.tile([P, E], F32)
-            copy(out=out_sb[:], in_=o_ps[:])
-            nc.sync.dma_start(out=out[r].rearrange("(m s) e -> m s e", s=QUERY_TILES)[:, s, :], in_=out_sb[:])
+            copy(out=out_tiles[r][:, s, :], in_=o_ps[:])
+            nc.sync.dma_start(
+                out=out[r].rearrange("(m s) e -> m s e", s=QUERY_TILES)[:, s, :], in_=out_tiles[r][:, s, :]
+            )
 
         for r in range(BEHIND, R):
             more_x = r + AHEAD < R

@@ -36,7 +36,6 @@ def tile_rowselfattention_pb_t_kernel(tc, attn_weights, mask0, x, Wv, bv, out):
         psum_x = ctx.enter_context(tc.psum_pool(name="psum_x", bufs=X_BANKS))
         psum_v = ctx.enter_context(tc.psum_pool(name="psum_v", bufs=3))
         psum_o = ctx.enter_context(tc.psum_pool(name="psum_o", bufs=3))
-        ctx.enter_context(tc.manual_schedule())
 
         ident_f32 = const.tile([P, P], F32)
         make_identity(nc, ident_f32[:])
@@ -151,15 +150,13 @@ def tile_rowselfattention_pb_t_kernel(tc, attn_weights, mask0, x, Wv, bv, out):
             nc.sync.dma_start(out=bias_row[0:1, :], in_=bv.rearrange("(o e) -> o e", o=1))
             nc.scalar.activation(out=one[:], in_=zero[:], func=ACT.Exp)
             attn_tiles = {}
-            halves = [slice(0, QUERY_TILES // 2), slice(QUERY_TILES // 2, QUERY_TILES)]
 
             def load_attn(h):
                 attn_sb = attn_pool.tile([P, QUERY_TILES, C], BF16)
-                for part in halves:
-                    nc.sync.dma_start(
-                        out=attn_sb[:, part, :],
-                        in_=attn_weights[h].rearrange("(m s) j -> m s j", s=QUERY_TILES)[:, part, :],
-                    )
+                nc.sync.dma_start(
+                    out=attn_sb[:].rearrange("m s j -> m (s j)"),
+                    in_=attn_weights[h].rearrange("(m s) j -> m (s j)", s=QUERY_TILES),
+                )
                 attn_tiles[h] = attn_sb
 
             load_attn(0)
@@ -200,6 +197,7 @@ def tile_rowselfattention_pb_t_kernel(tc, attn_weights, mask0, x, Wv, bv, out):
             def softmax_max(h):
                 cols = slice(h * QUERY_TILES, (h + 1) * QUERY_TILES)
                 attn_sb = attn_tiles[h]
+                halves = [slice(0, QUERY_TILES // 2), slice(QUERY_TILES // 2, QUERY_TILES)]
                 half_max = max_pool.tile([P, QUERY_TILES, C // 2], BF16)
                 for part in halves:
                     nc.vector.tensor_max(
@@ -216,11 +214,10 @@ def tile_rowselfattention_pb_t_kernel(tc, attn_weights, mask0, x, Wv, bv, out):
                     nc.vector.tensor_reduce(
                         out=row_max[:, cols][:, part], in_=quarter_max[:, part], axis=AXIS.X, op=ALU.max
                     )
-                for part in halves:
-                    nc.vector.scalar_tensor_tensor(
-                        out=shift[:, cols][:, part], in0=row_max[:, cols][:, part], scalar=-1.0, in1=keep[:, part],
-                        op0=ALU.mult, op1=ALU.mult,
-                    )
+                nc.vector.scalar_tensor_tensor(
+                    out=shift[:, cols], in0=row_max[:, cols], scalar=-1.0, in1=keep[:],
+                    op0=ALU.mult, op1=ALU.mult,
+                )
 
             def softmax_exp(h):
                 for s in range(QUERY_TILES):
@@ -299,14 +296,10 @@ def tile_rowselfattention_pb_t_kernel(tc, attn_weights, mask0, x, Wv, bv, out):
                 if 0 <= k - 3 < BEHIND:
                     v_quantise(k - 3)
 
-        out_pool = ctx.enter_context(tc.tile_pool(name="out_pool", bufs=4))
-        out_tiles = {}
+        out_pool = ctx.enter_context(tc.tile_pool(name="out_pool", bufs=12))
 
         def attend_bank(bank, copy):
             r, s = divmod(bank, QUERY_TILES)
-            if s == 0:
-                out_sb = out_pool.tile([P, QUERY_TILES, E], F32)
-                out_tiles[r] = out_sb
             v_codes, v_scales = v_mx_tiles[r]
             o_ps = psum_o.tile([P, E], F32)
             for h in range(H):
@@ -321,10 +314,9 @@ def tile_rowselfattention_pb_t_kernel(tc, attn_weights, mask0, x, Wv, bv, out):
                     start=True,
                     stop=True,
                 )
-            copy(out=out_tiles[r][:, s, :], in_=o_ps[:])
-            nc.sync.dma_start(
-                out=out[r].rearrange("(m s) e -> m s e", s=QUERY_TILES)[:, s, :], in_=out_tiles[r][:, s, :]
-            )
+            out_sb = out_pool.tile([P, E], F32)
+            copy(out=out_sb[:], in_=o_ps[:])
+            nc.sync.dma_start(out=out[r].rearrange("(m s) e -> m s e", s=QUERY_TILES)[:, s, :], in_=out_sb[:])
 
         for r in range(BEHIND, R):
             more_x = r + AHEAD < R

@@ -10,7 +10,6 @@ U8 = mybir.dt.uint8
 FP8X4 = mybir.dt.float8_e4m3fn_x4
 ALU = mybir.AluOpType
 ACT = mybir.ActivationFunctionType
-AXIS = mybir.AxisListType
 
 P = 128
 PACK = 4
@@ -39,8 +38,6 @@ def tile_rowselfattention_pb_t_kernel(tc, attn_weights, mask0, x, Wv, bv, out):
 
         ident_f32 = const.tile([P, P], F32)
         make_identity(nc, ident_f32[:])
-        ident_bf16 = const.tile([P, P], BF16)
-        make_identity(nc, ident_bf16[:])
         ones = const.tile([P, P], BF16)
         nc.vector.memset(ones[:], 1.0)
         bias_row = const.tile([P, E], BF16)
@@ -56,7 +53,7 @@ def tile_rowselfattention_pb_t_kernel(tc, attn_weights, mask0, x, Wv, bv, out):
         p_scales = const.tile([P, H * C], U8, align_bytes=64)
         mask_sb = const.tile([P, QUERY_TILES], BF16)
         keep = const.tile([P, QUERY_TILES], F32)
-        row_max = const.tile([P, H * QUERY_TILES], F32)
+        minus_keep = const.tile([P, QUERY_TILES], F32)
         shift = const.tile([P, H * QUERY_TILES], F32)
         row_sum = const.tile([P, H * QUERY_TILES], F32)
         inv_sum = const.tile([P, H * QUERY_TILES], F32)
@@ -190,42 +187,29 @@ def tile_rowselfattention_pb_t_kernel(tc, attn_weights, mask0, x, Wv, bv, out):
             nc.vector.tensor_scalar(
                 out=keep[:], in0=mask_sb[:], scalar1=-1.0, scalar2=1.0, op0=ALU.mult, op1=ALU.add
             )
+            nc.vector.tensor_scalar(
+                out=minus_keep[:], in0=mask_sb[:], scalar1=-1.0, scalar2=None, op0=ALU.add
+            )
             exp_tiles = {}
             p_ps_tiles = {}
             p_grouped_tiles = {}
 
             def softmax_max(h):
-                cols = slice(h * QUERY_TILES, (h + 1) * QUERY_TILES)
-                attn_sb = attn_tiles[h]
-                halves = [slice(0, QUERY_TILES // 2), slice(QUERY_TILES // 2, QUERY_TILES)]
-                half_max = max_pool.tile([P, QUERY_TILES, C // 2], BF16)
-                for part in halves:
-                    nc.vector.tensor_max(
-                        out=half_max[:, part], in0=attn_sb[:, part, 0 : C // 2], in1=attn_sb[:, part, C // 2 : C]
+                for s in range(QUERY_TILES):
+                    col = h * QUERY_TILES + s
+                    product = max_pool.tile([P, C], BF16)
+                    nc.vector.tensor_scalar(
+                        out=product[:], in0=attn_tiles[h][:, s, :], scalar1=minus_keep[:, s : s + 1],
+                        scalar2=None, op0=ALU.mult, op1=ALU.min, accum_out=shift[:, col : col + 1],
                     )
-                quarter_max = max_pool.tile([P, QUERY_TILES, C // 4], BF16)
-                for part in halves:
-                    nc.vector.tensor_max(
-                        out=quarter_max[:, part],
-                        in0=half_max[:, part, 0 : C // 4],
-                        in1=half_max[:, part, C // 4 : C // 2],
-                    )
-                for part in halves:
-                    nc.vector.tensor_reduce(
-                        out=row_max[:, cols][:, part], in_=quarter_max[:, part], axis=AXIS.X, op=ALU.max
-                    )
-                nc.vector.scalar_tensor_tensor(
-                    out=shift[:, cols], in0=row_max[:, cols], scalar=-1.0, in1=keep[:],
-                    op0=ALU.mult, op1=ALU.mult,
-                )
 
             def softmax_exp(h):
                 for s in range(QUERY_TILES):
                     col = h * QUERY_TILES + s
-                    exp_sb = exp_pool.tile([P, PACK, P], F32)
+                    exp_sb = exp_pool.tile([P, 2, P, 2], F32)
                     nc.scalar.activation(
                         out=exp_sb[:],
-                        in_=attn_tiles[h][:, s, :].rearrange("m (q t) -> m t q", t=PACK),
+                        in_=attn_tiles[h][:, s, :].rearrange("m (q u e) -> m u q e", u=2, e=2),
                         func=ACT.Exp,
                         bias=shift[:, col : col + 1],
                         scale=keep[:, s : s + 1],
@@ -239,23 +223,27 @@ def tile_rowselfattention_pb_t_kernel(tc, attn_weights, mask0, x, Wv, bv, out):
                 p_ps_tiles[h] = []
                 for s in range(QUERY_TILES):
                     col = h * QUERY_TILES + s
-                    p_sb = p_pool.tile([P, PACK, P], BF16)
+                    p_sb = p_pool.tile([P, 2 * P * 2], BF16)
                     nc.vector.tensor_scalar(
-                        out=p_sb[:], in0=exp_tiles[(h, s)][:], scalar1=inv_sum[:, col : col + 1],
+                        out=p_sb[:], in0=exp_tiles[(h, s)][:].rearrange("m u q e -> m (u q e)"), scalar1=inv_sum[:, col : col + 1],
                         scalar2=None, op0=ALU.mult,
                     )
                     if s % 2 == 0:
-                        p_ps = psum_o.tile([P, 2, PACK, P], BF16, tag="o_ps")
+                        p_ps = psum_o.tile([P, 2, 2, P], F32, tag="o_ps")
                         p_ps_tiles[h].append(p_ps)
-                    for t in range(PACK):
-                        nc.tensor.transpose(p_ps_tiles[h][s // 2][:, s % 2, t, :], p_sb[:, t, :], ident_bf16[:])
+                    words = p_sb[:].bitcast(F32)
+                    for u in range(2):
+                        nc.tensor.transpose(
+                            p_ps_tiles[h][s // 2][:, s % 2, u, :], words[:, u * P : (u + 1) * P], ident_f32[:]
+                        )
 
             def softmax_evacuate(h):
-                p_grouped = p_stage.tile([P, QUERY_TILES, P, PACK], BF16, align_bytes=64)
+                p_grouped = p_stage.tile([P, QUERY_TILES * P * PACK], BF16, align_bytes=64)
+                grouped_words = p_grouped[:].bitcast(F32).rearrange("q (s m u) -> q s m u", s=QUERY_TILES, u=2)
                 for pair in range(QUERY_TILES // 2):
                     nc.scalar.copy(
-                        out=p_grouped[:, 2 * pair : 2 * pair + 2],
-                        in_=p_ps_tiles[h][pair][:].rearrange("q s t m -> q s m t"),
+                        out=grouped_words[:, 2 * pair : 2 * pair + 2],
+                        in_=p_ps_tiles[h][pair][:].rearrange("q s u m -> q s m u"),
                     )
                 p_grouped_tiles[h] = p_grouped
 
@@ -264,7 +252,7 @@ def tile_rowselfattention_pb_t_kernel(tc, attn_weights, mask0, x, Wv, bv, out):
                 nc.vector.quantize_mx(
                     out=p_codes[:, cols].bitcast(FP8X4),
                     scales=p_scales[:, cols],
-                    in_=p_grouped_tiles[h][:].rearrange("q s m t -> q (s m t)"),
+                    in_=p_grouped_tiles[h][:],
                 )
 
             first_rows = AHEAD + BEHIND

@@ -17,8 +17,8 @@ R, C, E, H = 16, 512, 512, 4
 D = E // H
 QUERY_TILES = C // P
 X_BANKS = 2
-AHEAD = 2
-BEHIND = 2
+BANKS_A_STEP = 5
+LAG = 2
 
 FLOPS = 2 * R * C * E * E + 2 * H * C * C * R * D
 
@@ -29,12 +29,20 @@ def tile_rowselfattention_pb_t_kernel(tc, attn_weights, mask0, x, Wv, bv, out):
         const = ctx.enter_context(tc.tile_pool(name="const", bufs=1))
         x_pool = ctx.enter_context(tc.tile_pool(name="x_pool", bufs=R))
         x_stage = ctx.enter_context(tc.tile_pool(name="x_stage", bufs=3))
-        x_mx = ctx.enter_context(tc.tile_pool(name="x_mx", bufs=AHEAD + 2))
+        x_mx = ctx.enter_context(tc.tile_pool(name="x_mx", bufs=3))
         v_stage = ctx.enter_context(tc.tile_pool(name="v_stage", bufs=3))
-        v_mx = ctx.enter_context(tc.tile_pool(name="v_mx", bufs=BEHIND + 2))
+        v_mx = ctx.enter_context(tc.tile_pool(name="v_mx", bufs=6))
+        out_pool = ctx.enter_context(tc.tile_pool(name="out_pool", bufs=5))
+        attn_pool = ctx.enter_context(tc.tile_pool(name="attn_pool", bufs=H))
+        w_pool = ctx.enter_context(tc.tile_pool(name="w_pool", bufs=1))
+        product_pool = ctx.enter_context(tc.tile_pool(name="product_pool", bufs=2))
+        exp_pool = ctx.enter_context(tc.tile_pool(name="exp_pool", bufs=2 * QUERY_TILES))
+        p_pool = ctx.enter_context(tc.tile_pool(name="p_pool", bufs=QUERY_TILES))
+        p_stage = ctx.enter_context(tc.tile_pool(name="p_stage", bufs=2))
         psum_x = ctx.enter_context(tc.psum_pool(name="psum_x", bufs=X_BANKS))
         psum_v = ctx.enter_context(tc.psum_pool(name="psum_v", bufs=3))
         psum_o = ctx.enter_context(tc.psum_pool(name="psum_o", bufs=3))
+        ctx.enter_context(tc.manual_schedule())
 
         ident_f32 = const.tile([P, P], F32)
         make_identity(nc, ident_f32[:])
@@ -58,15 +66,46 @@ def tile_rowselfattention_pb_t_kernel(tc, attn_weights, mask0, x, Wv, bv, out):
         row_sum = const.tile([P, H * QUERY_TILES], F32)
         inv_sum = const.tile([P, H * QUERY_TILES], F32)
 
+        attn_tiles = {}
         x_tiles = {}
-        x_ps_tiles = {}
-        x_grouped_tiles = {}
-        x_mx_tiles = {}
+
+        def load_attn(h, first, count):
+            if first == 0:
+                attn_sb = attn_pool.tile([P, QUERY_TILES, C], BF16)
+                attn_tiles[h] = attn_sb
+            part = slice(first, first + count)
+            nc.sync.dma_start(
+                out=attn_tiles[h][:, part], in_=attn_weights[h].rearrange("(m s) j -> m s j", s=QUERY_TILES)[:, part]
+            )
 
         def load_x(r):
             x_sb = x_pool.tile([P, PACK * E], BF16)
             nc.sync.dma_start(out=x_sb[:], in_=x[r].rearrange("(q t) f -> q (t f)", t=PACK))
             x_tiles[r] = x_sb
+
+        nc.sync.dma_start(out=mask_sb[:], in_=mask0.rearrange("(m s) -> m s", s=QUERY_TILES))
+        nc.scalar.activation(out=one[:], in_=zero[:], func=ACT.Exp)
+        load_attn(0, 0, 2)
+        w_rows = w_pool.tile([P, PACK, E], BF16)
+        nc.sync.dma_start(
+            out=w_rows[:].rearrange("w (u e) n -> w u (e n)", u=2),
+            in_=Wv.rearrange("(u w e) n -> w u (e n)", u=2, e=2),
+        )
+        load_attn(0, 2, 2)
+        load_x(0)
+        nc.sync.dma_start(out=bias_row[0:1, :], in_=bv.rearrange("(o e) -> o e", o=1))
+        load_attn(1, 0, QUERY_TILES)
+        load_x(1)
+        load_attn(2, 0, QUERY_TILES)
+        load_x(2)
+        load_attn(3, 0, QUERY_TILES)
+        load_x(3)
+        for r in range(H, R):
+            load_x(r)
+
+        x_ps_tiles = {}
+        x_grouped_tiles = {}
+        x_mx_tiles = {}
 
         def x_transpose(r):
             words = x_tiles[r][:].bitcast(F32)
@@ -125,208 +164,195 @@ def tile_rowselfattention_pb_t_kernel(tc, attn_weights, mask0, x, Wv, bv, out):
                 op=ALU.add,
             )
 
-        def v_quantise(r):
-            v_codes = v_mx.tile([P, E], U32, align_bytes=64)
-            v_scales = v_mx.tile([P, E], U8, align_bytes=64)
+        def v_quantise(r, first, count):
+            v_codes = v_mx.tile([P, count * D], U32, align_bytes=64)
+            v_scales = v_mx.tile([P, count * D], U8, align_bytes=64)
             nc.vector.quantize_mx(
                 out=v_codes[:].bitcast(FP8X4),
                 scales=v_scales[:],
-                in_=v_grouped_tiles[r][:].rearrange("q h d t -> q (h d t)"),
+                in_=v_grouped_tiles[r][:, first : first + count].rearrange("q h d t -> q (h d t)"),
             )
-            v_mx_tiles[r] = (v_codes, v_scales)
+            for h in range(count):
+                v_mx_tiles[(r, first + h)] = (v_codes[:, h * D : (h + 1) * D], v_scales[:, h * D : (h + 1) * D])
 
-        with ExitStack() as start:
-            attn_pool = start.enter_context(tc.tile_pool(name="attn_pool", bufs=H))
-            w_pool = start.enter_context(tc.tile_pool(name="w_pool", bufs=1))
-            max_pool = start.enter_context(tc.tile_pool(name="max_pool", bufs=2))
-            exp_pool = start.enter_context(tc.tile_pool(name="exp_pool", bufs=2 * QUERY_TILES))
-            p_pool = start.enter_context(tc.tile_pool(name="p_pool", bufs=2 * QUERY_TILES))
-            p_stage = start.enter_context(tc.tile_pool(name="p_stage", bufs=H))
-
-            nc.sync.dma_start(out=mask_sb[:], in_=mask0.rearrange("(m s) -> m s", s=QUERY_TILES))
-            nc.sync.dma_start(out=bias_row[0:1, :], in_=bv.rearrange("(o e) -> o e", o=1))
-            nc.scalar.activation(out=one[:], in_=zero[:], func=ACT.Exp)
-            attn_tiles = {}
-
-            def load_attn(h):
-                attn_sb = attn_pool.tile([P, QUERY_TILES, C], BF16)
-                nc.sync.dma_start(
-                    out=attn_sb[:].rearrange("m s j -> m (s j)"),
-                    in_=attn_weights[h].rearrange("(m s) j -> m (s j)", s=QUERY_TILES),
-                )
-                attn_tiles[h] = attn_sb
-
-            load_attn(0)
-            load_attn(1)
-            w_rows = w_pool.tile([P, PACK, E], BF16)
-            nc.sync.dma_start(
-                out=w_rows[:].rearrange("w (u e) n -> w u (e n)", u=2),
-                in_=Wv.rearrange("(u w e) n -> w u (e n)", u=2, e=2),
+        def group_weights():
+            w_grouped = w_pool.tile([P, E, PACK], BF16, align_bytes=64)
+            nc.gpsimd.tensor_scalar(
+                out=w_grouped[:], in0=w_rows[:].rearrange("w t n -> w n t"),
+                scalar1=1.0, scalar2=0.0, op0=ALU.mult, op1=ALU.add,
             )
-            load_x(0)
-            load_x(1)
-            load_attn(2)
-            load_attn(3)
-            for r in range(2, R):
-                load_x(r)
+            return w_grouped
 
-            def prepare_weights():
-                w_grouped = w_pool.tile([P, E, PACK], BF16, align_bytes=64)
-                nc.vector.tensor_copy(out=w_grouped[:], in_=w_rows[:].rearrange("w t n -> w n t"))
-                nc.vector.quantize_mx(
-                    out=w_codes[:].bitcast(FP8X4),
-                    scales=w_scales[:],
-                    in_=w_grouped[:].rearrange("w n t -> w (n t)"),
+        def quantise_weights(w_grouped):
+            nc.vector.quantize_mx(
+                out=w_codes[:].bitcast(FP8X4),
+                scales=w_scales[:],
+                in_=w_grouped[:].rearrange("w n t -> w (n t)"),
+            )
+
+        def prepare_bias():
+            bias_ps = psum_v.tile([P, E], F32, tag="v_ps")
+            nc.tensor.matmul(out=bias_ps[:], lhsT=ones[:], rhs=bias_row[:], start=True, stop=True)
+            nc.scalar.copy(out=bias_sb[:], in_=bias_ps[:])
+
+        nc.vector.tensor_scalar(
+            out=keep[:], in0=mask_sb[:], scalar1=-1.0, scalar2=1.0, op0=ALU.mult, op1=ALU.add
+        )
+        nc.vector.tensor_scalar(
+            out=minus_keep[:], in0=mask_sb[:], scalar1=-1.0, scalar2=None, op0=ALU.add
+        )
+        exp_tiles = {}
+        p_tiles = {}
+        p_ps_tiles = {}
+        p_grouped_tiles = {}
+
+        def softmax_max(h):
+            for s in range(QUERY_TILES):
+                col = h * QUERY_TILES + s
+                product = product_pool.tile([P, C], BF16)
+                nc.vector.tensor_scalar(
+                    out=product[:], in0=attn_tiles[h][:, s, :], scalar1=minus_keep[:, s : s + 1],
+                    scalar2=None, op0=ALU.mult, op1=ALU.min, accum_out=shift[:, col : col + 1],
                 )
 
-            def prepare_bias():
-                bias_ps = psum_v.tile([P, E], F32, tag="v_ps")
-                nc.tensor.matmul(out=bias_ps[:], lhsT=ones[:], rhs=bias_row[:], start=True, stop=True)
-                nc.scalar.copy(out=bias_sb[:], in_=bias_ps[:])
-
-            nc.vector.tensor_scalar(
-                out=keep[:], in0=mask_sb[:], scalar1=-1.0, scalar2=1.0, op0=ALU.mult, op1=ALU.add
-            )
-            nc.vector.tensor_scalar(
-                out=minus_keep[:], in0=mask_sb[:], scalar1=-1.0, scalar2=None, op0=ALU.add
-            )
-            exp_tiles = {}
-            p_ps_tiles = {}
-            p_grouped_tiles = {}
-
-            def softmax_max(h):
-                for s in range(QUERY_TILES):
-                    col = h * QUERY_TILES + s
-                    product = max_pool.tile([P, C], BF16)
-                    nc.vector.tensor_scalar(
-                        out=product[:], in0=attn_tiles[h][:, s, :], scalar1=minus_keep[:, s : s + 1],
-                        scalar2=None, op0=ALU.mult, op1=ALU.min, accum_out=shift[:, col : col + 1],
-                    )
-
-            def softmax_exp(h):
-                for s in range(QUERY_TILES):
-                    col = h * QUERY_TILES + s
-                    exp_sb = exp_pool.tile([P, 2, P, 2], F32)
-                    nc.scalar.activation(
-                        out=exp_sb[:],
-                        in_=attn_tiles[h][:, s, :].rearrange("m (q u e) -> m u q e", u=2, e=2),
-                        func=ACT.Exp,
-                        bias=shift[:, col : col + 1],
-                        scale=keep[:, s : s + 1],
-                        accum_out=row_sum[:, col : col + 1],
-                    )
-                    exp_tiles[(h, s)] = exp_sb
-
-            def softmax_transpose(h):
-                cols = slice(h * QUERY_TILES, (h + 1) * QUERY_TILES)
-                nc.vector.reciprocal(out=inv_sum[:, cols], in_=row_sum[:, cols])
-                p_ps_tiles[h] = []
-                for s in range(QUERY_TILES):
-                    col = h * QUERY_TILES + s
-                    p_sb = p_pool.tile([P, 2 * P * 2], BF16)
-                    nc.vector.tensor_scalar(
-                        out=p_sb[:], in0=exp_tiles[(h, s)][:].rearrange("m u q e -> m (u q e)"), scalar1=inv_sum[:, col : col + 1],
-                        scalar2=None, op0=ALU.mult,
-                    )
-                    if s % 2 == 0:
-                        p_ps = psum_o.tile([P, 2, 2, P], F32, tag="o_ps")
-                        p_ps_tiles[h].append(p_ps)
-                    words = p_sb[:].bitcast(F32)
-                    for u in range(2):
-                        nc.tensor.transpose(
-                            p_ps_tiles[h][s // 2][:, s % 2, u, :], words[:, u * P : (u + 1) * P], ident_f32[:]
-                        )
-
-            def softmax_evacuate(h):
-                p_grouped = p_stage.tile([P, QUERY_TILES * P * PACK], BF16, align_bytes=64)
-                grouped_words = p_grouped[:].bitcast(F32).rearrange("q (s m u) -> q s m u", s=QUERY_TILES, u=2)
-                for pair in range(QUERY_TILES // 2):
-                    nc.scalar.copy(
-                        out=grouped_words[:, 2 * pair : 2 * pair + 2],
-                        in_=p_ps_tiles[h][pair][:].rearrange("q s u m -> q s m u"),
-                    )
-                p_grouped_tiles[h] = p_grouped
-
-            def softmax_quantise(h):
-                cols = slice(h * C, (h + 1) * C)
-                nc.vector.quantize_mx(
-                    out=p_codes[:, cols].bitcast(FP8X4),
-                    scales=p_scales[:, cols],
-                    in_=p_grouped_tiles[h][:],
+        def softmax_exp(h):
+            for s in range(QUERY_TILES):
+                col = h * QUERY_TILES + s
+                exp_sb = exp_pool.tile([P, 2, P, 2], F32)
+                nc.scalar.activation(
+                    out=exp_sb[:],
+                    in_=attn_tiles[h][:, s, :].rearrange("m (q u e) -> m u q e", u=2, e=2),
+                    func=ACT.Exp,
+                    bias=shift[:, col : col + 1],
+                    scale=keep[:, s : s + 1],
+                    accum_out=row_sum[:, col : col + 1],
                 )
+                exp_tiles[(h, s)] = exp_sb
 
-            first_rows = AHEAD + BEHIND
-            softmax_max(0)
-            softmax_max(1)
-            prepare_bias()
-            prepare_weights()
-            x_transpose(0)
-            for k in range(H + 3):
-                if 0 <= k - 2 < H:
-                    softmax_evacuate(k - 2)
-                if k < H:
-                    softmax_exp(k)
-                if k < first_rows:
-                    x_evacuate(k)
-                if 0 <= k - 1 < H:
-                    softmax_transpose(k - 1)
-                if 2 <= k + 1 < H:
-                    softmax_max(k + 1)
-                if 0 <= k - 1 < first_rows:
-                    x_quantise(k - 1)
-                if 0 <= k - 2 < BEHIND:
-                    for h in range(H):
-                        project_bank(k - 2, h)
-                if k + 1 < first_rows:
-                    x_transpose(k + 1)
-                if 0 <= k - 3 < H:
-                    softmax_quantise(k - 3)
-                if 0 <= k - 3 < BEHIND:
-                    v_quantise(k - 3)
+        def softmax_scale(h):
+            cols = slice(h * QUERY_TILES, (h + 1) * QUERY_TILES)
+            nc.vector.reciprocal(out=inv_sum[:, cols], in_=row_sum[:, cols])
+            for s in range(QUERY_TILES):
+                col = h * QUERY_TILES + s
+                p_sb = p_pool.tile([P, 2 * P * 2], BF16)
+                nc.gpsimd.tensor_scalar(
+                    out=p_sb[:], in0=exp_tiles[(h, s)][:].rearrange("m u q e -> m (u q e)"),
+                    scalar1=inv_sum[:, col : col + 1], scalar2=0.0, op0=ALU.mult, op1=ALU.add,
+                )
+                p_tiles[(h, s)] = p_sb
 
-        out_pool = ctx.enter_context(tc.tile_pool(name="out_pool", bufs=12))
+        def softmax_transpose(h):
+            p_ps_tiles[h] = []
+            for s in range(QUERY_TILES):
+                if s % 2 == 0:
+                    p_ps = psum_o.tile([P, 2, 2, P], F32, tag="o_ps")
+                    p_ps_tiles[h].append(p_ps)
+                words = p_tiles[(h, s)][:].bitcast(F32)
+                for u in range(2):
+                    nc.tensor.transpose(
+                        p_ps_tiles[h][s // 2][:, s % 2, u, :], words[:, u * P : (u + 1) * P], ident_f32[:]
+                    )
 
-        def attend_bank(bank, copy):
-            r, s = divmod(bank, QUERY_TILES)
-            v_codes, v_scales = v_mx_tiles[r]
-            o_ps = psum_o.tile([P, E], F32)
-            for h in range(H):
+        def softmax_evacuate(h):
+            p_grouped = p_stage.tile([P, QUERY_TILES * P * PACK], BF16, align_bytes=64)
+            grouped_words = p_grouped[:].bitcast(F32).rearrange("q (s m u) -> q s m u", s=QUERY_TILES, u=2)
+            for pair in range(QUERY_TILES // 2):
+                nc.scalar.copy(
+                    out=grouped_words[:, 2 * pair : 2 * pair + 2],
+                    in_=p_ps_tiles[h][pair][:].rearrange("q s u m -> q s m u"),
+                )
+            p_grouped_tiles[h] = p_grouped
+
+        def softmax_quantise(h):
+            cols = slice(h * C, (h + 1) * C)
+            nc.vector.quantize_mx(
+                out=p_codes[:, cols].bitcast(FP8X4),
+                scales=p_scales[:, cols],
+                in_=p_grouped_tiles[h][:],
+            )
+
+        out_tiles = {}
+
+        def attend_bank(r, h, copy):
+            v_codes, v_scales = v_mx_tiles[(r, h)]
+            o_ps = psum_o.tile([P, QUERY_TILES, D], F32)
+            for s in range(QUERY_TILES):
                 queries = slice((h * QUERY_TILES + s) * P, (h * QUERY_TILES + s + 1) * P)
-                head = slice(h * D, (h + 1) * D)
                 nc.tensor.matmul_mx(
-                    out=o_ps[:, head],
+                    out=o_ps[:, s, :],
                     lhsT=p_codes[:, queries].bitcast(FP8X4),
                     lhsT_scale=p_scales[:, queries],
-                    rhs=v_codes[:, head].bitcast(FP8X4),
-                    rhs_scale=v_scales[:, head],
+                    rhs=v_codes.bitcast(FP8X4),
+                    rhs_scale=v_scales,
                     start=True,
                     stop=True,
                 )
-            out_sb = out_pool.tile([P, E], F32)
-            copy(out=out_sb[:], in_=o_ps[:])
-            nc.sync.dma_start(out=out[r].rearrange("(m s) e -> m s e", s=QUERY_TILES)[:, s, :], in_=out_sb[:])
+            if h == 0:
+                out_sb = out_pool.tile([P, QUERY_TILES, E], F32)
+                out_tiles[r] = out_sb
+            copy(out=out_tiles[r][:, :, h * D : (h + 1) * D], in_=o_ps[:])
 
-        for r in range(BEHIND, R):
-            more_x = r + AHEAD < R
-            bank = QUERY_TILES * (r - BEHIND) + X_BANKS * max(0, r + AHEAD - R)
-            if more_x:
-                x_transpose(r + AHEAD)
-            project_bank(r, 0)
-            if more_x:
-                x_evacuate(r + AHEAD)
-            else:
-                for spare in range(X_BANKS):
-                    attend_bank(bank, nc.scalar.copy)
-                    bank += 1
-            for h in range(1, H + 1):
-                if h < H:
-                    project_bank(r, h)
-                attend_bank(bank, nc.scalar.copy)
-                bank += 1
-            if more_x:
-                x_quantise(r + AHEAD)
-            v_quantise(r)
+        def store(r, first, count):
+            cols = slice(first * D, (first + count) * D)
+            nc.sync.dma_start(
+                out=out[r].rearrange("(m s) e -> m s e", s=QUERY_TILES)[:, :, cols],
+                in_=out_tiles[r][:, :, cols],
+            )
 
-        for s in range(QUERY_TILES):
-            copy = nc.scalar.copy if s % 2 == 0 else nc.vector.tensor_copy
-            attend_bank(QUERY_TILES * (R - 1) + s, copy)
+        w_grouped = group_weights()
+        softmax_max(0)
+        x_transpose(0)
+        waiting = []
+        for k in range(R + 1):
+            waiting += [(r, h) for r in range(R) for h in range(H) if max(r, h) + LAG == k]
+            banks = waiting[:BANKS_A_STEP]
+            waiting = waiting[BANKS_A_STEP:]
+            if k < H:
+                softmax_exp(k)
+            if k == 0:
+                prepare_bias()
+            if k < R:
+                x_evacuate(k)
+            if 0 <= k - 1 < R:
+                x_quantise(k - 1)
+            if 0 <= k - 2 < R:
+                v_quantise(k - 2, 0, H)
+            if 0 <= k - 2 < H:
+                softmax_quantise(k - 2)
+            if 0 <= k - 1 < R:
+                project_bank(k - 1, 0)
+                project_bank(k - 1, 1)
+            if k < H:
+                softmax_scale(k)
+            if k == 0:
+                quantise_weights(w_grouped)
+            if k + 1 < H:
+                softmax_max(k + 1)
+            if 0 <= k - 1 < H:
+                softmax_transpose(k - 1)
+                softmax_evacuate(k - 1)
+            for r, h in banks[:1]:
+                attend_bank(r, h, nc.scalar.copy)
+            if k == R:
+                v_quantise(R - 1, 0, H // 2)
+            if 0 <= k - 1 < R:
+                project_bank(k - 1, 2)
+            for r, h in banks[1:2]:
+                attend_bank(r, h, nc.scalar.copy)
+            if 0 <= k - 1 < R:
+                project_bank(k - 1, 3)
+            for r, h in banks[2:]:
+                attend_bank(r, h, nc.scalar.copy)
+            for r, h in banks:
+                if h == H - 1:
+                    store(r, 0, H)
+            if k + 1 < R:
+                x_transpose(k + 1)
+        v_quantise(R - 1, H // 2, H // 2)
+        waiting += [(R - 1, h) for h in range(H)]
+        for n, (r, h) in enumerate(waiting):
+            attend_bank(r, h, nc.scalar.copy if n % 2 == 0 else nc.vector.tensor_copy)
+            if r < R - 1 and h == H - 1:
+                store(r, 0, H)
+            if r == R - 1 and h % 2 == 1:
+                store(r, h - 1, 2)

@@ -46,7 +46,7 @@ def tile_rowselfattention_pb_t_kernel(tc, attn_weights, mask0, x, Wv, bv, out):
 
         ident_f32 = const.tile([P, P], F32)
         make_identity(nc, ident_f32[:])
-        ones = const.tile([P, P], BF16)
+        ones = const.tile([P, E], BF16)
         nc.vector.memset(ones[:], 1.0)
         bias_row = const.tile([P, E], BF16)
         nc.vector.memset(bias_row[:], 0.0)
@@ -92,8 +92,8 @@ def tile_rowselfattention_pb_t_kernel(tc, attn_weights, mask0, x, Wv, bv, out):
             in_=Wv.rearrange("(u w e) n -> w u (e n)", u=2, e=2),
         )
         load_attn(0, 2, 2)
-        load_x(0)
         nc.sync.dma_start(out=bias_row[0:1, :], in_=bv.rearrange("(o e) -> o e", o=1))
+        load_x(0)
         load_attn(1, 0, QUERY_TILES)
         load_x(1)
         load_attn(2, 0, QUERY_TILES)
@@ -192,7 +192,7 @@ def tile_rowselfattention_pb_t_kernel(tc, attn_weights, mask0, x, Wv, bv, out):
 
         def prepare_bias():
             bias_ps = psum_v.tile([P, E], F32, tag="v_ps")
-            nc.tensor.matmul(out=bias_ps[:], lhsT=ones[:], rhs=bias_row[:], start=True, stop=True)
+            nc.tensor.matmul(out=bias_ps[:], lhsT=ones[:, :P], rhs=bias_row[:], start=True, stop=True)
             nc.scalar.copy(out=bias_sb[:], in_=bias_ps[:])
 
         nc.vector.tensor_scalar(
@@ -206,8 +206,8 @@ def tile_rowselfattention_pb_t_kernel(tc, attn_weights, mask0, x, Wv, bv, out):
         p_ps_tiles = {}
         p_grouped_tiles = {}
 
-        def softmax_max(h):
-            for s in range(QUERY_TILES):
+        def softmax_max(h, first, count):
+            for s in range(first, first + count):
                 col = h * QUERY_TILES + s
                 product = product_pool.tile([P, C], BF16)
                 nc.vector.tensor_scalar(
@@ -300,59 +300,71 @@ def tile_rowselfattention_pb_t_kernel(tc, attn_weights, mask0, x, Wv, bv, out):
             )
 
         w_grouped = group_weights()
-        softmax_max(0)
+        softmax_max(0, 0, QUERY_TILES)
         x_transpose(0)
         waiting = []
         for k in range(R + 1):
             waiting += [(r, h) for r in range(R) for h in range(H) if max(r, h) + LAG == k]
-            banks = waiting[:BANKS_A_STEP]
-            waiting = waiting[BANKS_A_STEP:]
+            cap = 4 if k < R else 4 + X_BANKS
+            banks = waiting[:cap]
+            waiting = waiting[cap:]
+            before = 0 if k <= H + 1 else 2 if k < R else 3
+            if 0 <= k - 1 < R:
+                x_quantise(k - 1)
             if k < H:
                 softmax_exp(k)
             if k == 0:
+                x_evacuate(0)
                 prepare_bias()
-            if k < R:
-                x_evacuate(k)
-            if 0 <= k - 1 < R:
-                x_quantise(k - 1)
+                softmax_scale(0)
+                quantise_weights(w_grouped)
+                softmax_max(1, 0, 4)
             if 0 <= k - 2 < R:
                 v_quantise(k - 2, 0, H)
+            if 1 < k < H:
+                softmax_scale(k)
             if 0 <= k - 2 < H:
                 softmax_quantise(k - 2)
+            for r, h in banks[:before]:
+                attend_bank(r, h, nc.scalar.copy)
+            if 0 < k < R:
+                x_evacuate(k)
+            if 1 < k <= H:
+                softmax_transpose(k - 1)
+                softmax_evacuate(k - 1)
             if 0 <= k - 1 < R:
                 project_bank(k - 1, 0)
                 project_bank(k - 1, 1)
-            if k < H:
+            if k == 1:
                 softmax_scale(k)
-            if k == 0:
-                quantise_weights(w_grouped)
-            if k + 1 < H:
-                softmax_max(k + 1)
-            if 0 <= k - 1 < H:
+            if 1 < k + 1 < H:
+                softmax_max(k + 1, 0, QUERY_TILES)
+            if k == 1:
                 softmax_transpose(k - 1)
                 softmax_evacuate(k - 1)
-            for r, h in banks[:1]:
-                attend_bank(r, h, nc.scalar.copy)
-            if k == R:
-                v_quantise(R - 1, 0, H // 2)
             if 0 <= k - 1 < R:
                 project_bank(k - 1, 2)
-            for r, h in banks[1:2]:
+            if k == R:
+                v_quantise(R - 1, 0, 2)
+            for r, h in banks[before:before + 1]:
                 attend_bank(r, h, nc.scalar.copy)
             if 0 <= k - 1 < R:
                 project_bank(k - 1, 3)
-            for r, h in banks[2:]:
+            for r, h in banks[before + 1:]:
                 attend_bank(r, h, nc.scalar.copy)
             for r, h in banks:
                 if h == H - 1:
                     store(r, 0, H)
             if k + 1 < R:
                 x_transpose(k + 1)
-        v_quantise(R - 1, H // 2, H // 2)
+        v_quantise(R - 1, 2, 1)
+        v_quantise(R - 1, 3, 1)
         waiting += [(R - 1, h) for h in range(H)]
         for n, (r, h) in enumerate(waiting):
             attend_bank(r, h, nc.scalar.copy if n % 2 == 0 else nc.vector.tensor_copy)
             if r < R - 1 and h == H - 1:
                 store(r, 0, H)
-            if r == R - 1 and h % 2 == 1:
-                store(r, h - 1, 2)
+            if r == R - 1 and h == 1:
+                store(r, 0, 2)
+            if r == R - 1 and h > 1:
+                store(r, h, 1)

@@ -18,6 +18,7 @@ D = E // H
 QUERY_TILES = C // P
 X_BANKS = 2
 BANKS_A_STEP = 5
+HEAD_ROWS = 4
 LAG = 2
 
 FLOPS = 2 * R * C * E * E + 2 * H * C * C * R * D
@@ -273,38 +274,47 @@ def tile_rowselfattention_pb_t_kernel(tc, attn_weights, mask0, x, Wv, bv, out):
 
         out_tiles = {}
 
-        def attend_bank(r, h, copy):
-            v_codes, v_scales = v_mx_tiles[(r, h)]
-            o_ps = psum_o.tile([P, QUERY_TILES, D], F32)
-            for s in range(QUERY_TILES):
-                queries = slice((h * QUERY_TILES + s) * P, (h * QUERY_TILES + s + 1) * P)
-                nc.tensor.matmul_mx(
-                    out=o_ps[:, s, :],
-                    lhsT=p_codes[:, queries].bitcast(FP8X4),
-                    lhsT_scale=p_scales[:, queries],
-                    rhs=v_codes.bitcast(FP8X4),
-                    rhs_scale=v_scales,
-                    start=True,
-                    stop=True,
-                )
-            if h == 0:
+        def attend_bank(bank, copy):
+            r, tiles, heads = bank
+            o_ps = psum_o.tile([P, len(tiles), len(heads) * D], F32)
+            for s in tiles:
+                for h in heads:
+                    v_codes, v_scales = v_mx_tiles[(r, h)]
+                    queries = slice((h * QUERY_TILES + s) * P, (h * QUERY_TILES + s + 1) * P)
+                    nc.tensor.matmul_mx(
+                        out=o_ps[:, s - tiles[0], (h - heads[0]) * D : (h - heads[0] + 1) * D],
+                        lhsT=p_codes[:, queries].bitcast(FP8X4),
+                        lhsT_scale=p_scales[:, queries],
+                        rhs=v_codes.bitcast(FP8X4),
+                        rhs_scale=v_scales,
+                        start=True,
+                        stop=True,
+                    )
+            if r not in out_tiles:
                 out_sb = out_pool.tile([P, QUERY_TILES, E], F32)
                 out_tiles[r] = out_sb
-            copy(out=out_tiles[r][:, :, h * D : (h + 1) * D], in_=o_ps[:])
+            rows = slice(tiles[0], tiles[-1] + 1)
+            copy(out=out_tiles[r][:, rows, heads[0] * D : (heads[-1] + 1) * D], in_=o_ps[:])
+            if heads[-1] == H - 1:
+                nc.sync.dma_start(
+                    out=out[r].rearrange("(m s) e -> m s e", s=QUERY_TILES)[:, rows], in_=out_tiles[r][:, rows]
+                )
 
-        def store(r, first, count):
-            cols = slice(first * D, (first + count) * D)
-            nc.sync.dma_start(
-                out=out[r].rearrange("(m s) e -> m s e", s=QUERY_TILES)[:, :, cols],
-                in_=out_tiles[r][:, :, cols],
-            )
+        def banks_of(r):
+            size = QUERY_TILES if r < HEAD_ROWS else 1 if r < R - 1 else 2
+            per = QUERY_TILES // size
+            return [
+                (r, list(range(s, s + size)), list(range(h, h + per)))
+                for h in range(0, H, per)
+                for s in range(0, QUERY_TILES, size)
+            ]
 
         w_grouped = group_weights()
         softmax_max(0, 0, QUERY_TILES)
         x_transpose(0)
         waiting = []
         for k in range(R + 1):
-            waiting += [(r, h) for r in range(R) for h in range(H) if max(r, h) + LAG == k]
+            waiting += [bank for r in range(R) for bank in banks_of(r) if max(r, bank[2][-1]) + LAG == k]
             cap = 4 if k < R else 4 + X_BANKS
             banks = waiting[:cap]
             waiting = waiting[cap:]
@@ -325,8 +335,8 @@ def tile_rowselfattention_pb_t_kernel(tc, attn_weights, mask0, x, Wv, bv, out):
                 softmax_scale(k)
             if 0 <= k - 2 < H:
                 softmax_quantise(k - 2)
-            for r, h in banks[:before]:
-                attend_bank(r, h, nc.scalar.copy)
+            for bank in banks[:before]:
+                attend_bank(bank, nc.scalar.copy)
             if 0 < k < R:
                 x_evacuate(k)
             if 1 < k <= H:
@@ -346,25 +356,15 @@ def tile_rowselfattention_pb_t_kernel(tc, attn_weights, mask0, x, Wv, bv, out):
                 project_bank(k - 1, 2)
             if k == R:
                 v_quantise(R - 1, 0, 2)
-            for r, h in banks[before:before + 1]:
-                attend_bank(r, h, nc.scalar.copy)
+            for bank in banks[before:before + 1]:
+                attend_bank(bank, nc.scalar.copy)
             if 0 <= k - 1 < R:
                 project_bank(k - 1, 3)
-            for r, h in banks[before + 1:]:
-                attend_bank(r, h, nc.scalar.copy)
-            for r, h in banks:
-                if h == H - 1:
-                    store(r, 0, H)
+            for bank in banks[before + 1:]:
+                attend_bank(bank, nc.scalar.copy)
             if k + 1 < R:
                 x_transpose(k + 1)
-        v_quantise(R - 1, 2, 1)
-        v_quantise(R - 1, 3, 1)
-        waiting += [(R - 1, h) for h in range(H)]
-        for n, (r, h) in enumerate(waiting):
-            attend_bank(r, h, nc.scalar.copy if n % 2 == 0 else nc.vector.tensor_copy)
-            if r < R - 1 and h == H - 1:
-                store(r, 0, H)
-            if r == R - 1 and h == 1:
-                store(r, 0, 2)
-            if r == R - 1 and h > 1:
-                store(r, h, 1)
+        v_quantise(R - 1, 2, 2)
+        waiting += banks_of(R - 1)
+        for n, bank in enumerate(waiting):
+            attend_bank(bank, nc.scalar.copy if n % 2 == 0 else nc.vector.tensor_copy)

@@ -18,8 +18,8 @@ D = E // H
 QUERY_TILES = C // P
 X_BANKS = 2
 BANKS_A_STEP = 5
+LAG = 3
 HEAD_ROWS = 4
-LAG = 2
 
 FLOPS = 2 * R * C * E * E + 2 * H * C * C * R * D
 
@@ -315,56 +315,52 @@ def tile_rowselfattention_pb_t_kernel(tc, attn_weights, mask0, x, Wv, bv, out):
         waiting = []
         for k in range(R + 1):
             waiting += [bank for r in range(R) for bank in banks_of(r) if max(r, bank[2][-1]) + LAG == k]
-            cap = 4 if k < R else 4 + X_BANKS
+            cap = 4 if k < R - 2 else 5 if k < R else 8
             banks = waiting[:cap]
             waiting = waiting[cap:]
-            before = 0 if k <= H + 1 else 2 if k < R else 3
-            if 0 <= k - 1 < R:
-                x_quantise(k - 1)
             if k < H:
                 softmax_exp(k)
+            if k < R:
+                x_evacuate(k)
             if k == 0:
-                x_evacuate(0)
                 prepare_bias()
                 softmax_scale(0)
                 quantise_weights(w_grouped)
                 softmax_max(1, 0, 4)
-            if 0 <= k - 2 < R:
-                v_quantise(k - 2, 0, H)
-            if 1 < k < H:
-                softmax_scale(k)
             if 0 <= k - 2 < H:
                 softmax_quantise(k - 2)
-            for bank in banks[:before]:
-                attend_bank(bank, nc.scalar.copy)
-            if 0 < k < R:
-                x_evacuate(k)
-            if 1 < k <= H:
-                softmax_transpose(k - 1)
-                softmax_evacuate(k - 1)
             if 0 <= k - 1 < R:
                 project_bank(k - 1, 0)
+            for bank in banks[:1]:
+                attend_bank(bank, nc.scalar.copy)
+            if 0 <= k - 2 < R:
+                v_quantise(k - 2, 0, H)
+            if 0 <= k - 1 < R:
                 project_bank(k - 1, 1)
-            if k == 1:
+            if 0 < k < H:
                 softmax_scale(k)
+            for bank in banks[1:2]:
+                attend_bank(bank, nc.scalar.copy)
+            if k < R:
+                x_quantise(k)
             if 1 < k + 1 < H:
                 softmax_max(k + 1, 0, QUERY_TILES)
-            if k == 1:
+            if 0 < k <= H:
                 softmax_transpose(k - 1)
                 softmax_evacuate(k - 1)
             if 0 <= k - 1 < R:
                 project_bank(k - 1, 2)
             if k == R:
                 v_quantise(R - 1, 0, 2)
-            for bank in banks[before:before + 1]:
+            for bank in banks[2:3]:
                 attend_bank(bank, nc.scalar.copy)
             if 0 <= k - 1 < R:
                 project_bank(k - 1, 3)
-            for bank in banks[before + 1:]:
+            for bank in banks[3:]:
                 attend_bank(bank, nc.scalar.copy)
             if k + 1 < R:
                 x_transpose(k + 1)
         v_quantise(R - 1, 2, 2)
-        waiting += banks_of(R - 1)
+        waiting += [bank for r in range(R - 3, R) for bank in banks_of(r) if r + LAG > R]
         for n, bank in enumerate(waiting):
             attend_bank(bank, nc.scalar.copy if n % 2 == 0 else nc.vector.tensor_copy)

@@ -18,7 +18,6 @@ D = E // H
 QUERY_TILES = C // P
 X_BANKS = 2
 BANKS_A_STEP = 5
-LAG = 3
 HEAD_ROWS = 4
 
 FLOPS = 2 * R * C * E * E + 2 * H * C * C * R * D
@@ -274,9 +273,9 @@ def tile_rowselfattention_pb_t_kernel(tc, attn_weights, mask0, x, Wv, bv, out):
 
         out_tiles = {}
 
-        def attend_bank(bank, copy):
+        def attend_bank(bank, copy, pool, tag):
             r, tiles, heads = bank
-            o_ps = psum_o.tile([P, len(tiles), len(heads) * D], F32)
+            o_ps = pool.tile([P, len(tiles), len(heads) * D], F32, tag=tag)
             for s in tiles:
                 for h in heads:
                     v_codes, v_scales = v_mx_tiles[(r, h)]
@@ -295,9 +294,11 @@ def tile_rowselfattention_pb_t_kernel(tc, attn_weights, mask0, x, Wv, bv, out):
                 out_tiles[r] = out_sb
             rows = slice(tiles[0], tiles[-1] + 1)
             copy(out=out_tiles[r][:, rows, heads[0] * D : (heads[-1] + 1) * D], in_=o_ps[:])
-            if heads[-1] == H - 1:
+            if r == R - 1 or heads[-1] == H - 1:
+                cols = slice(heads[0] * D, (heads[-1] + 1) * D) if r == R - 1 else slice(0, E)
                 nc.sync.dma_start(
-                    out=out[r].rearrange("(m s) e -> m s e", s=QUERY_TILES)[:, rows], in_=out_tiles[r][:, rows]
+                    out=out[r].rearrange("(m s) e -> m s e", s=QUERY_TILES)[:, rows, cols],
+                    in_=out_tiles[r][:, rows, cols],
                 )
 
         def banks_of(r):
@@ -314,8 +315,8 @@ def tile_rowselfattention_pb_t_kernel(tc, attn_weights, mask0, x, Wv, bv, out):
         x_transpose(0)
         waiting = []
         for k in range(R + 1):
-            waiting += [bank for r in range(R) for bank in banks_of(r) if max(r, bank[2][-1]) + LAG == k]
-            cap = 4 if k < R - 2 else 5 if k < R else 8
+            waiting += [bank for r in range(R) for bank in banks_of(r) if max(r + (2 if r >= R - 2 else 3), bank[2][-1] + 3) == k]
+            cap = 4 if k < R - 2 else 6
             banks = waiting[:cap]
             waiting = waiting[cap:]
             if k < H:
@@ -332,7 +333,7 @@ def tile_rowselfattention_pb_t_kernel(tc, attn_weights, mask0, x, Wv, bv, out):
             if 0 <= k - 1 < R:
                 project_bank(k - 1, 0)
             for bank in banks[:1]:
-                attend_bank(bank, nc.scalar.copy)
+                attend_bank(bank, nc.scalar.copy, psum_o, "o_ps")
             if 0 <= k - 2 < R:
                 v_quantise(k - 2, 0, H)
             if 0 <= k - 1 < R:
@@ -340,7 +341,7 @@ def tile_rowselfattention_pb_t_kernel(tc, attn_weights, mask0, x, Wv, bv, out):
             if 0 < k < H:
                 softmax_scale(k)
             for bank in banks[1:2]:
-                attend_bank(bank, nc.scalar.copy)
+                attend_bank(bank, nc.scalar.copy, psum_o, "o_ps")
             if k < R:
                 x_quantise(k)
             if 1 < k + 1 < H:
@@ -353,14 +354,17 @@ def tile_rowselfattention_pb_t_kernel(tc, attn_weights, mask0, x, Wv, bv, out):
             if k == R:
                 v_quantise(R - 1, 0, 2)
             for bank in banks[2:3]:
-                attend_bank(bank, nc.scalar.copy)
+                attend_bank(bank, nc.scalar.copy, psum_o, "o_ps")
             if 0 <= k - 1 < R:
                 project_bank(k - 1, 3)
             for bank in banks[3:]:
-                attend_bank(bank, nc.scalar.copy)
+                attend_bank(bank, nc.scalar.copy, psum_o, "o_ps")
             if k + 1 < R:
                 x_transpose(k + 1)
         v_quantise(R - 1, 2, 2)
-        waiting += [bank for r in range(R - 3, R) for bank in banks_of(r) if r + LAG > R]
+        waiting += [bank for r in range(R - 3, R) for bank in banks_of(r) if r + (2 if r >= R - 2 else 3) > R]
         for n, bank in enumerate(waiting):
-            attend_bank(bank, nc.scalar.copy if n % 2 == 0 else nc.vector.tensor_copy)
+            if n % 2 == 0:
+                attend_bank(bank, nc.scalar.copy, psum_o, "o_ps")
+            else:
+                attend_bank(bank, nc.vector.tensor_copy, psum_v, "v_ps")

@@ -294,11 +294,9 @@ def tile_rowselfattention_pb_t_kernel(tc, attn_weights, mask0, x, Wv, bv, out):
                 out_tiles[r] = out_sb
             rows = slice(tiles[0], tiles[-1] + 1)
             copy(out=out_tiles[r][:, rows, heads[0] * D : (heads[-1] + 1) * D], in_=o_ps[:])
-            if r == R - 1 or heads[-1] == H - 1:
-                cols = slice(heads[0] * D, (heads[-1] + 1) * D) if r == R - 1 else slice(0, E)
+            if heads[-1] == H - 1:
                 nc.sync.dma_start(
-                    out=out[r].rearrange("(m s) e -> m s e", s=QUERY_TILES)[:, rows, cols],
-                    in_=out_tiles[r][:, rows, cols],
+                    out=out[r].rearrange("(m s) e -> m s e", s=QUERY_TILES)[:, rows], in_=out_tiles[r][:, rows]
                 )
 
         def banks_of(r):
@@ -328,8 +326,8 @@ def tile_rowselfattention_pb_t_kernel(tc, attn_weights, mask0, x, Wv, bv, out):
                 softmax_scale(0)
                 quantise_weights(w_grouped)
                 softmax_max(1, 0, 4)
-            if 0 <= k - 2 < H:
-                softmax_quantise(k - 2)
+            if 1 < k + 1 < H:
+                softmax_max(k + 1, 0, QUERY_TILES)
             if 0 <= k - 1 < R:
                 project_bank(k - 1, 0)
             for bank in banks[:1]:
@@ -344,13 +342,13 @@ def tile_rowselfattention_pb_t_kernel(tc, attn_weights, mask0, x, Wv, bv, out):
                 attend_bank(bank, nc.scalar.copy, psum_o, "o_ps")
             if k < R:
                 x_quantise(k)
-            if 1 < k + 1 < H:
-                softmax_max(k + 1, 0, QUERY_TILES)
+            if 0 <= k - 1 < R:
+                project_bank(k - 1, 2)
+            if 0 <= k - 2 < H:
+                softmax_quantise(k - 2)
             if 0 < k <= H:
                 softmax_transpose(k - 1)
                 softmax_evacuate(k - 1)
-            if 0 <= k - 1 < R:
-                project_bank(k - 1, 2)
             if k == R:
                 v_quantise(R - 1, 0, 2)
             for bank in banks[2:3]:

@@ -85,13 +85,14 @@ def tile_rowselfattention_pb_t_kernel(tc, attn_weights, mask0, x, Wv, bv, out):
 
         nc.sync.dma_start(out=mask_sb[:], in_=mask0.rearrange("(m s) -> m s", s=QUERY_TILES))
         nc.scalar.activation(out=one[:], in_=zero[:], func=ACT.Exp)
-        load_attn(0, 0, 2)
+        load_attn(0, 0, 1)
+        load_attn(0, 1, 1)
+        load_attn(0, 2, 2)
         w_rows = w_pool.tile([P, PACK, E], BF16)
         nc.sync.dma_start(
             out=w_rows[:].rearrange("w (u e) n -> w u (e n)", u=2),
             in_=Wv.rearrange("(u w e) n -> w u (e n)", u=2, e=2),
         )
-        load_attn(0, 2, 2)
         nc.sync.dma_start(out=bias_row[0:1, :], in_=bv.rearrange("(o e) -> o e", o=1))
         load_x(0)
         load_attn(1, 0, QUERY_TILES)
@@ -177,10 +178,7 @@ def tile_rowselfattention_pb_t_kernel(tc, attn_weights, mask0, x, Wv, bv, out):
 
         def group_weights():
             w_grouped = w_pool.tile([P, E, PACK], BF16, align_bytes=64)
-            nc.gpsimd.tensor_scalar(
-                out=w_grouped[:], in0=w_rows[:].rearrange("w t n -> w n t"),
-                scalar1=1.0, scalar2=0.0, op0=ALU.mult, op1=ALU.add,
-            )
+            nc.vector.tensor_copy(out=w_grouped[:], in_=w_rows[:].rearrange("w t n -> w n t"))
             return w_grouped
 
         def quantise_weights(w_grouped):
@@ -308,13 +306,13 @@ def tile_rowselfattention_pb_t_kernel(tc, attn_weights, mask0, x, Wv, bv, out):
                 for s in range(0, QUERY_TILES, size)
             ]
 
-        w_grouped = group_weights()
         softmax_max(0, 0, QUERY_TILES)
+        w_grouped = group_weights()
         x_transpose(0)
         waiting = []
         for k in range(R + 1):
             waiting += [bank for r in range(R) for bank in banks_of(r) if max(r + (2 if r >= R - 2 else 3), bank[2][-1] + 3) == k]
-            cap = 4 if k < R - 2 else 6
+            cap = 4 if k < R - 3 else 5 if k < R - 1 else 6
             banks = waiting[:cap]
             waiting = waiting[cap:]
             if k < H:

from contextlib import ExitStack

import concourse.mybir as mybir
from concourse.masks import make_identity

F32 = mybir.dt.float32
BF16 = mybir.dt.bfloat16
U32 = mybir.dt.uint32
U8 = mybir.dt.uint8
FP8X4 = mybir.dt.float8_e4m3fn_x4
ALU = mybir.AluOpType
ACT = mybir.ActivationFunctionType

P = 128
PACK = 4
R, C, E, H = 16, 512, 512, 4
D = E // H
QUERY_TILES = C // P
X_BANKS = 2
BANKS_A_STEP = 5
HEAD_ROWS = 4

FLOPS = 2 * R * C * E * E + 2 * H * C * C * R * D


def tile_rowselfattention_pb_t_kernel(tc, attn_weights, mask0, x, Wv, bv, out):
    nc = tc.nc
    with ExitStack() as ctx:
        const = ctx.enter_context(tc.tile_pool(name="const", bufs=1))
        x_pool = ctx.enter_context(tc.tile_pool(name="x_pool", bufs=R))
        x_stage = ctx.enter_context(tc.tile_pool(name="x_stage", bufs=3))
        x_mx = ctx.enter_context(tc.tile_pool(name="x_mx", bufs=3))
        v_stage = ctx.enter_context(tc.tile_pool(name="v_stage", bufs=3))
        v_mx = ctx.enter_context(tc.tile_pool(name="v_mx", bufs=6))
        out_pool = ctx.enter_context(tc.tile_pool(name="out_pool", bufs=5))
        attn_pool = ctx.enter_context(tc.tile_pool(name="attn_pool", bufs=H))
        w_pool = ctx.enter_context(tc.tile_pool(name="w_pool", bufs=1))
        product_pool = ctx.enter_context(tc.tile_pool(name="product_pool", bufs=2))
        exp_pool = ctx.enter_context(tc.tile_pool(name="exp_pool", bufs=2 * QUERY_TILES))
        p_pool = ctx.enter_context(tc.tile_pool(name="p_pool", bufs=QUERY_TILES))
        p_stage = ctx.enter_context(tc.tile_pool(name="p_stage", bufs=2))
        psum_x = ctx.enter_context(tc.psum_pool(name="psum_x", bufs=X_BANKS))
        psum_v = ctx.enter_context(tc.psum_pool(name="psum_v", bufs=3))
        psum_o = ctx.enter_context(tc.psum_pool(name="psum_o", bufs=3))
        ctx.enter_context(tc.manual_schedule())

        ident_f32 = const.tile([P, P], F32)
        make_identity(nc, ident_f32[:])
        ones = const.tile([P, E], BF16)
        nc.vector.memset(ones[:], 1.0)
        bias_row = const.tile([P, E], BF16)
        nc.vector.memset(bias_row[:], 0.0)
        zero = const.tile([P, 1], F32)
        nc.vector.memset(zero[:], 0.0)
        one = const.tile([P, 1], F32)

        bias_sb = const.tile([P, E], F32)
        w_codes = const.tile([P, E], U32, align_bytes=64)
        w_scales = const.tile([P, E], U8, align_bytes=64)
        p_codes = const.tile([P, H * C], U32, align_bytes=64)
        p_scales = const.tile([P, H * C], U8, align_bytes=64)
        mask_sb = const.tile([P, QUERY_TILES], BF16)
        keep = const.tile([P, QUERY_TILES], F32)
        minus_keep = const.tile([P, QUERY_TILES], F32)
        shift = const.tile([P, H * QUERY_TILES], F32)
        row_sum = const.tile([P, H * QUERY_TILES], F32)
        inv_sum = const.tile([P, H * QUERY_TILES], F32)

        attn_tiles = {}
        x_tiles = {}

        def load_attn(h, first, count):
            if first == 0:
                attn_sb = attn_pool.tile([P, QUERY_TILES, C], BF16)
                attn_tiles[h] = attn_sb
            part = slice(first, first + count)
            nc.sync.dma_start(
                out=attn_tiles[h][:, part], in_=attn_weights[h].rearrange("(m s) j -> m s j", s=QUERY_TILES)[:, part]
            )

        def load_x(r):
            x_sb = x_pool.tile([P, PACK * E], BF16)
            nc.sync.dma_start(out=x_sb[:], in_=x[r].rearrange("(q t) f -> q (t f)", t=PACK))
            x_tiles[r] = x_sb

        nc.sync.dma_start(out=mask_sb[:], in_=mask0.rearrange("(m s) -> m s", s=QUERY_TILES))
        nc.scalar.activation(out=one[:], in_=zero[:], func=ACT.Exp)
        load_attn(0, 0, 1)
        load_attn(0, 1, 1)
        load_attn(0, 2, 2)
        w_rows = w_pool.tile([P, PACK, E], BF16)
        nc.sync.dma_start(
            out=w_rows[:].rearrange("w (u e) n -> w u (e n)", u=2),
            in_=Wv.rearrange("(u w e) n -> w u (e n)", u=2, e=2),
        )
        nc.sync.dma_start(out=bias_row[0:1, :], in_=bv.rearrange("(o e) -> o e", o=1))
        load_x(0)
        load_attn(1, 0, QUERY_TILES)
        load_x(1)
        load_attn(2, 0, QUERY_TILES)
        load_x(2)
        load_attn(3, 0, QUERY_TILES)
        load_x(3)
        for r in range(H, R):
            load_x(r)

        x_ps_tiles = {}
        x_grouped_tiles = {}
        x_mx_tiles = {}

        def x_transpose(r):
            words = x_tiles[r][:].bitcast(F32)
            x_ps_tiles[r] = []
            for bank in range(X_BANKS):
                x_ps = psum_x.tile([P, 2, 2, P], F32)
                for t_in in range(2):
                    for u in range(2):
                        first = ((2 * bank + t_in) * 2 + u) * P
                        nc.tensor.transpose(x_ps[:, t_in, u, :], words[:, first : first + P], ident_f32[:])
                x_ps_tiles[r].append(x_ps)

        def x_evacuate(r):
            x_grouped = x_stage.tile([P, PACK * P * PACK], BF16, align_bytes=64)
            grouped_words = x_grouped[:].bitcast(F32).rearrange("w (t q u) -> w t q u", t=PACK, u=2)
            for bank in range(X_BANKS):
                nc.scalar.copy(
                    out=grouped_words[:, 2 * bank : 2 * bank + 2],
                    in_=x_ps_tiles[r][bank][:].rearrange("w t u q -> w t q u"),
                )
            x_grouped_tiles[r] = x_grouped

        def x_quantise(r):
            x_codes = x_mx.tile([P, PACK * P], U32, align_bytes=64)
            x_scales = x_mx.tile([P, PACK * P], U8, align_bytes=64)
            nc.vector.quantize_mx(
                out=x_codes[:].bitcast(FP8X4), scales=x_scales[:], in_=x_grouped_tiles[r][:]
            )
            x_mx_tiles[r] = (x_codes, x_scales)

        v_grouped_tiles = {}
        v_mx_tiles = {}

        def project_bank(r, h):
            if h == 0:
                v_grouped = v_stage.tile([P, H, D, PACK], BF16, align_bytes=64)
                v_grouped_tiles[r] = v_grouped
            x_codes, x_scales = x_mx_tiles[r]
            head = slice(h * D, (h + 1) * D)
            v_ps = psum_v.tile([P, PACK, D], F32)
            for t in range(PACK):
                cols = slice(t * P, (t + 1) * P)
                nc.tensor.matmul_mx(
                    out=v_ps[:, t, :],
                    lhsT=x_codes[:, cols].bitcast(FP8X4),
                    lhsT_scale=x_scales[:, cols],
                    rhs=w_codes[:, head].bitcast(FP8X4),
                    rhs_scale=w_scales[:, head],
                    start=True,
                    stop=True,
                )
            nc.vector.tensor_tensor(
                out=v_grouped_tiles[r][:, h],
                in0=v_ps[:].rearrange("q t d -> q d t"),
                in1=bias_sb[:, head].unsqueeze(2).to_broadcast([P, D, PACK]),
                op=ALU.add,
            )

        def v_quantise(r, first, count):
            v_codes = v_mx.tile([P, count * D], U32, align_bytes=64)
            v_scales = v_mx.tile([P, count * D], U8, align_bytes=64)
            nc.vector.quantize_mx(
                out=v_codes[:].bitcast(FP8X4),
                scales=v_scales[:],
                in_=v_grouped_tiles[r][:, first : first + count].rearrange("q h d t -> q (h d t)"),
            )
            for h in range(count):
                v_mx_tiles[(r, first + h)] = (v_codes[:, h * D : (h + 1) * D], v_scales[:, h * D : (h + 1) * D])

        def group_weights():
            w_grouped = w_pool.tile([P, E, PACK], BF16, align_bytes=64)
            nc.vector.tensor_copy(out=w_grouped[:], in_=w_rows[:].rearrange("w t n -> w n t"))
            return w_grouped

        def quantise_weights(w_grouped):
            nc.vector.quantize_mx(
                out=w_codes[:].bitcast(FP8X4),
                scales=w_scales[:],
                in_=w_grouped[:].rearrange("w n t -> w (n t)"),
            )

        def prepare_bias():
            bias_ps = psum_v.tile([P, E], F32, tag="v_ps")
            nc.tensor.matmul(out=bias_ps[:], lhsT=ones[:, :P], rhs=bias_row[:], start=True, stop=True)
            nc.scalar.copy(out=bias_sb[:], in_=bias_ps[:])

        nc.vector.tensor_scalar(
            out=keep[:], in0=mask_sb[:], scalar1=-1.0, scalar2=1.0, op0=ALU.mult, op1=ALU.add
        )
        nc.vector.tensor_scalar(
            out=minus_keep[:], in0=mask_sb[:], scalar1=-1.0, scalar2=None, op0=ALU.add
        )
        exp_tiles = {}
        p_tiles = {}
        p_ps_tiles = {}
        p_grouped_tiles = {}

        def softmax_max(h, first, count):
            for s in range(first, first + count):
                col = h * QUERY_TILES + s
                product = product_pool.tile([P, C], BF16)
                nc.vector.tensor_scalar(
                    out=product[:], in0=attn_tiles[h][:, s, :], scalar1=minus_keep[:, s : s + 1],
                    scalar2=None, op0=ALU.mult, op1=ALU.min, accum_out=shift[:, col : col + 1],
                )

        def softmax_exp(h):
            for s in range(QUERY_TILES):
                col = h * QUERY_TILES + s
                exp_sb = exp_pool.tile([P, 2, P, 2], F32)
                nc.scalar.activation(
                    out=exp_sb[:],
                    in_=attn_tiles[h][:, s, :].rearrange("m (q u e) -> m u q e", u=2, e=2),
                    func=ACT.Exp,
                    bias=shift[:, col : col + 1],
                    scale=keep[:, s : s + 1],
                    accum_out=row_sum[:, col : col + 1],
                )
                exp_tiles[(h, s)] = exp_sb

        def softmax_scale(h):
            cols = slice(h * QUERY_TILES, (h + 1) * QUERY_TILES)
            nc.vector.reciprocal(out=inv_sum[:, cols], in_=row_sum[:, cols])
            for s in range(QUERY_TILES):
                col = h * QUERY_TILES + s
                p_sb = p_pool.tile([P, 2 * P * 2], BF16)
                nc.gpsimd.tensor_scalar(
                    out=p_sb[:], in0=exp_tiles[(h, s)][:].rearrange("m u q e -> m (u q e)"),
                    scalar1=inv_sum[:, col : col + 1], scalar2=0.0, op0=ALU.mult, op1=ALU.add,
                )
                p_tiles[(h, s)] = p_sb

        def softmax_transpose(h):
            p_ps_tiles[h] = []
            for s in range(QUERY_TILES):
                if s % 2 == 0:
                    p_ps = psum_o.tile([P, 2, 2, P], F32, tag="o_ps")
                    p_ps_tiles[h].append(p_ps)
                words = p_tiles[(h, s)][:].bitcast(F32)
                for u in range(2):
                    nc.tensor.transpose(
                        p_ps_tiles[h][s // 2][:, s % 2, u, :], words[:, u * P : (u + 1) * P], ident_f32[:]
                    )

        def softmax_evacuate(h):
            p_grouped = p_stage.tile([P, QUERY_TILES * P * PACK], BF16, align_bytes=64)
            grouped_words = p_grouped[:].bitcast(F32).rearrange("q (s m u) -> q s m u", s=QUERY_TILES, u=2)
            for pair in range(QUERY_TILES // 2):
                nc.scalar.copy(
                    out=grouped_words[:, 2 * pair : 2 * pair + 2],
                    in_=p_ps_tiles[h][pair][:].rearrange("q s u m -> q s m u"),
                )
            p_grouped_tiles[h] = p_grouped

        def softmax_quantise(h):
            cols = slice(h * C, (h + 1) * C)
            nc.vector.quantize_mx(
                out=p_codes[:, cols].bitcast(FP8X4),
                scales=p_scales[:, cols],
                in_=p_grouped_tiles[h][:],
            )

        out_tiles = {}

        def attend_bank(bank, copy, pool, tag):
            r, tiles, heads = bank
            o_ps = pool.tile([P, len(tiles), len(heads) * D], F32, tag=tag)
            for s in tiles:
                for h in heads:
                    v_codes, v_scales = v_mx_tiles[(r, h)]
                    queries = slice((h * QUERY_TILES + s) * P, (h * QUERY_TILES + s + 1) * P)
                    nc.tensor.matmul_mx(
                        out=o_ps[:, s - tiles[0], (h - heads[0]) * D : (h - heads[0] + 1) * D],
                        lhsT=p_codes[:, queries].bitcast(FP8X4),
                        lhsT_scale=p_scales[:, queries],
                        rhs=v_codes.bitcast(FP8X4),
                        rhs_scale=v_scales,
                        start=True,
                        stop=True,
                    )
            if r not in out_tiles:
                out_sb = out_pool.tile([P, QUERY_TILES, E], F32)
                out_tiles[r] = out_sb
            rows = slice(tiles[0], tiles[-1] + 1)
            copy(out=out_tiles[r][:, rows, heads[0] * D : (heads[-1] + 1) * D], in_=o_ps[:])
            if heads[-1] == H - 1:
                nc.sync.dma_start(
                    out=out[r].rearrange("(m s) e -> m s e", s=QUERY_TILES)[:, rows], in_=out_tiles[r][:, rows]
                )

        def banks_of(r):
            size = QUERY_TILES if r < HEAD_ROWS else 1 if r < R - 1 else 2
            per = QUERY_TILES // size
            return [
                (r, list(range(s, s + size)), list(range(h, h + per)))
                for h in range(0, H, per)
                for s in range(0, QUERY_TILES, size)
            ]

        softmax_max(0, 0, QUERY_TILES)
        w_grouped = group_weights()
        x_transpose(0)
        waiting = []
        for k in range(R + 1):
            waiting += [bank for r in range(R) for bank in banks_of(r) if max(r + (2 if r >= R - 2 else 3), bank[2][-1] + 3) == k]
            cap = 4 if k < R - 3 else 5 if k < R - 1 else 6
            banks = waiting[:cap]
            waiting = waiting[cap:]
            if k < H:
                softmax_exp(k)
            if k < R:
                x_evacuate(k)
            if k == 0:
                prepare_bias()
                softmax_scale(0)
                quantise_weights(w_grouped)
                softmax_max(1, 0, 4)
            if 1 < k + 1 < H:
                softmax_max(k + 1, 0, QUERY_TILES)
            if 0 <= k - 1 < R:
                project_bank(k - 1, 0)
            for bank in banks[:1]:
                attend_bank(bank, nc.scalar.copy, psum_o, "o_ps")
            if 0 <= k - 2 < R:
                v_quantise(k - 2, 0, H)
            if 0 <= k - 1 < R:
                project_bank(k - 1, 1)
            if 0 < k < H:
                softmax_scale(k)
            for bank in banks[1:2]:
                attend_bank(bank, nc.scalar.copy, psum_o, "o_ps")
            if k < R:
                x_quantise(k)
            if 0 <= k - 1 < R:
                project_bank(k - 1, 2)
            if 0 <= k - 2 < H:
                softmax_quantise(k - 2)
            if 0 < k <= H:
                softmax_transpose(k - 1)
                softmax_evacuate(k - 1)
            if k == R:
                v_quantise(R - 1, 0, 2)
            for bank in banks[2:3]:
                attend_bank(bank, nc.scalar.copy, psum_o, "o_ps")
            if 0 <= k - 1 < R:
                project_bank(k - 1, 3)
            for bank in banks[3:]:
                attend_bank(bank, nc.scalar.copy, psum_o, "o_ps")
            if k + 1 < R:
                x_transpose(k + 1)
        v_quantise(R - 1, 2, 2)
        waiting += [bank for r in range(R - 3, R) for bank in banks_of(r) if r + (2 if r >= R - 2 else 3) > R]
        for n, bank in enumerate(waiting):
            if n % 2 == 0:
                attend_bank(bank, nc.scalar.copy, psum_o, "o_ps")
            else:
                attend_bank(bank, nc.vector.tensor_copy, psum_v, "v_ps")
